import numpy as np
import ml_dtypes


def mxq(x, axis, fmt="e4m3"):
    dtype, down = {"e4m3": (ml_dtypes.float8_e4m3fn, 7), "e5m2": (ml_dtypes.float8_e5m2, 14)}[fmt]
    v = np.moveaxis(np.asarray(x, np.float32).astype(ml_dtypes.bfloat16).astype(np.float64), axis, -1)
    blocks = v.reshape(v.shape[:-1] + (-1, 32))
    amax = np.abs(blocks).max(-1, keepdims=True)
    byte = np.maximum(np.where(amax > 0, np.frexp(amax)[1] - 1 + 127, 0) - down, 1)
    scale = np.exp2(byte - 127.0)
    codes = (blocks / scale).astype(np.float32).astype(dtype).astype(np.float64)
    return np.moveaxis((codes * scale).reshape(v.shape), -1, axis)


WIDE = False


def mx_kscale(k):
    if not WIDE:
        return np.ones(k)
    levels = np.array([10, -10, 5, -5, 0])
    a = np.random.permutation(np.resize(levels, k // 512 * 4)).reshape(k // 512, 4)
    idx = np.arange(k)
    return np.exp2(a[idx // 512, idx % 128 // 32])


BF16 = ml_dtypes.bfloat16


def bf(x):
    return np.asarray(x, np.float32).astype(BF16)


def f64(x):
    return np.asarray(x).astype(np.float64)


B, T, V, C, K, R = 8, 16, 32, 512, 512, 256


def setup_inputs():
    n = np.random.standard_normal
    s = mx_kscale(C)
    x = 0.7 * n((B, 1, V, C)) + 0.7 * n((B, T, V, C))
    return {
        "x": bf(x * s),
        "A": bf(np.eye(V) + 0.1 * n((K, V, V))),
        "lam": bf(0.25 + 0.1 * np.random.random(1)),
        "phi_w": bf(n((C, K)) / np.sqrt(C) / s[:, None]),
        "phi_b": bf(0.3 * n(K)),
        "theta_w": bf(n((C, K)) / np.sqrt(C) / s[:, None]),
        "theta_b": bf(0.3 * n(K)),
        "kappa_w": bf(n((K, K)) / np.sqrt(K)),
        "kappa_b": bf(0.3 * n(K)),
    }


def reference(x, A, lam, phi_w, phi_b, theta_w, theta_b, kappa_w, kappa_b):
    xq = mxq(f64(x), 3, "e4m3")
    phi_x = ((xq @ mxq(f64(phi_w), 0, "e4m3")) + f64(phi_b)).mean(axis=1)
    theta_x = ((xq @ mxq(f64(theta_w), 0, "e4m3")) + f64(theta_b)).mean(axis=1)
    F_ij = np.tanh(phi_x[:, :, None, :] - theta_x[:, None, :, :])
    A_hat = np.transpose((mxq(F_ij, 3, "e4m3") @ mxq(f64(kappa_w), 0, "e4m3")) + f64(kappa_b), (0, 3, 1, 2))
    return f64(A)[None] + f64(lam) * A_hat

@@ -1,0 +1,203 @@
+from contextlib import ExitStack
+
+import concourse.mybir as mybir
+from concourse.masks import make_identity
+
+F32 = mybir.dt.float32
+BF16 = mybir.dt.bfloat16
+U32 = mybir.dt.uint32
+U8 = mybir.dt.uint8
+FP8X4 = mybir.dt.float8_e4m3fn_x4
+ALU = mybir.AluOpType
+ACT = mybir.ActivationFunctionType
+
+BATCH, STEPS, JOINTS, WIDTH = 8, 16, 32, 512
+P = 128
+PACK = 4
+assert P * PACK == WIDTH
+
+GROUP = P // JOINTS
+N_GROUPS = BATCH // GROUP
+ROWS_STEPS = P // JOINTS
+HALF_STEPS = 2 * ROWS_STEPS
+HALF_JOINTS = JOINTS // 2
+PAIRS = HALF_JOINTS * JOINTS
+
+FLOPS = 2 * BATCH * STEPS * JOINTS * WIDTH * 2 * WIDTH + 2 * BATCH * JOINTS * JOINTS * WIDTH * WIDTH
+
+
+def tile_attgcn_pa_t_kernel(
+    tc, x, A, lam, phi_w, phi_b, theta_w, theta_b, kappa_w, kappa_b, out
+):
+    nc = tc.nc
+    with ExitStack() as stack:
+        keep = stack.enter_context(tc.tile_pool(name="keep", bufs=1))
+        x_pool = stack.enter_context(tc.tile_pool(name="x_rows", bufs=N_GROUPS * STEPS // ROWS_STEPS))
+        stage = stack.enter_context(tc.tile_pool(name="stage", bufs=2))
+        work = stack.enter_context(tc.tile_pool(name="work", bufs=3))
+        ps_xt = stack.enter_context(tc.psum_pool(name="ps_xt", bufs=2))
+        ps_sum = stack.enter_context(tc.psum_pool(name="ps_sum", bufs=1))
+        ps_acc = stack.enter_context(tc.psum_pool(name="ps_acc", bufs=4))
+
+        def load_weight(w, label):
+            raw = keep.tile([P, PACK, WIDTH], BF16, name="%s_raw" % label)
+            nc.sync.dma_start(out=raw[:], in_=w.rearrange("(p j) c -> p j c", j=PACK))
+            return raw
+
+        def load_x(g, s):
+            rows = x_pool.tile([P, GROUP, WIDTH], BF16)
+            nc.sync.dma_start(
+                out=rows[:],
+                in_=x[g * GROUP : (g + 1) * GROUP, s * ROWS_STEPS : (s + 1) * ROWS_STEPS].rearrange(
+                    "b t v f -> (t v) b f"
+                ),
+            )
+            return rows
+
+        def load_per_channel(vec, label):
+            narrow = keep.tile([P, PACK], BF16, name="%s_bf16" % label)
+            nc.scalar.dma_start(out=narrow[:], in_=vec.rearrange("(q m) -> q m", m=PACK))
+            wide = keep.tile([P, PACK], F32, name="%s_f32" % label)
+            nc.vector.tensor_copy(out=wide[:], in_=narrow[:])
+            return wide
+
+        ident = keep.tile([P, P], F32)
+        make_identity(nc, ident[:])
+
+        n_tiles = STEPS // ROWS_STEPS
+        phi_raw = load_weight(phi_w, "phi")
+        x_rows = {(0, s): load_x(0, s) for s in range(n_tiles)}
+        theta_raw = load_weight(theta_w, "theta")
+        for s in range(n_tiles):
+            x_rows[(1, s)] = load_x(1, s)
+        kappa_raw = load_weight(kappa_w, "kappa")
+        a_bf16 = keep.tile([P, PACK, JOINTS * JOINTS], BF16)
+        nc.sync.dma_start(out=a_bf16[:], in_=A.rearrange("(q m) u v -> q m (u v)", m=PACK))
+
+        phi_bias = load_per_channel(phi_b, "phi_b")
+        theta_bias = load_per_channel(theta_b, "theta_b")
+        kappa_bias = load_per_channel(kappa_b, "kappa_b")
+        lam_bf16 = keep.tile([P, 1], BF16)
+        nc.scalar.dma_start(out=lam_bf16[:], in_=lam.partition_broadcast(P))
+        lam_col = keep.tile([P, 1], F32)
+        nc.vector.tensor_copy(out=lam_col[:], in_=lam_bf16[:])
+
+        def quantise_weight(raw, label):
+            grouped = stage.tile([P, PACK, P, PACK], BF16, align_bytes=64, tag="w_grouped")
+            nc.vector.tensor_copy(out=grouped[:], in_=raw[:].rearrange("p j (q m) -> p m q j", m=PACK))
+            codes = keep.tile([P, PACK, P], U32, align_bytes=64, name="%s_codes" % label)
+            scales = keep.tile([P, PACK, P], U8, align_bytes=64, name="%s_scales" % label)
+            nc.vector.quantize_mx(
+                out=codes[:].rearrange("p m q -> p (m q)").bitcast(FP8X4),
+                scales=scales[:].rearrange("p m q -> p (m q)"),
+                in_=grouped[:].rearrange("p m q j -> p (m q j)"),
+            )
+            return codes, scales
+
+        phi_q = quantise_weight(phi_raw, "phi")
+        theta_q = quantise_weight(theta_raw, "theta")
+
+        def mean_over_time(weight_q, bias, x_codes, x_scales, kind, g):
+            w_codes, w_scales = weight_q
+            sums = ps_sum.tile([P, PACK, P], F32, tag="%s_sums" % kind)
+            for m in range(PACK):
+                for t in range(STEPS):
+                    nc.tensor.matmul_mx(
+                        out=sums[:, m, :],
+                        lhsT=w_codes[:, m, :].bitcast(FP8X4),
+                        lhsT_scale=w_scales[:, m, :],
+                        rhs=x_codes[:, t, :].bitcast(FP8X4),
+                        rhs_scale=x_scales[:, t, :],
+                        start=(t == 0),
+                        stop=(t == STEPS - 1),
+                    )
+            mean = keep.tile([P, P, PACK], F32, name="%s_mean%d" % (kind, g))
+            nc.vector.scalar_tensor_tensor(
+                out=mean[:],
+                in0=sums[:].rearrange("p m c -> p c m"),
+                scalar=1.0 / STEPS,
+                in1=bias[:].unsqueeze(1).to_broadcast([P, P, PACK]),
+                op0=ALU.mult,
+                op1=ALU.add,
+            )
+            return mean
+
+        p_mean, th_mean = [], []
+        for g in range(N_GROUPS):
+            x_codes = keep.tile([P, STEPS, P], U32, align_bytes=64, name="x_codes%d" % g)
+            x_scales = keep.tile([P, STEPS, P], U8, align_bytes=64, name="x_scales%d" % g)
+            for h in range(STEPS // HALF_STEPS):
+                grouped = stage.tile([P, HALF_STEPS, GROUP, JOINTS, PACK], BF16, align_bytes=64, tag="x_grouped")
+                grouped_flat = grouped[:].rearrange("p t b v j -> p (t b v j)")
+                grouped_words = grouped_flat.bitcast(F32).rearrange(
+                    "p (t b v i) -> p t b v i", t=HALF_STEPS, b=GROUP, v=JOINTS
+                )
+                for b in range(GROUP):
+                    xt = ps_xt.tile([P, 2, 2, P], F32)
+                    for s in range(2):
+                        words = x_rows[(g, 2 * h + s)][:, b, :].bitcast(F32).rearrange("p (w i) -> p i w", i=2)
+                        for i in range(2):
+                            nc.tensor.transpose(xt[:, i, s, :], words[:, i, :], ident[:])
+                    nc.scalar.copy(
+                        out=grouped_words[:, :, b, :, :],
+                        in_=xt[:].rearrange("p i s (t v) -> p (s t) v i", v=JOINTS),
+                    )
+                steps = slice(h * HALF_STEPS, (h + 1) * HALF_STEPS)
+                nc.vector.quantize_mx(
+                    out=x_codes[:, steps, :].rearrange("p t c -> p (t c)").bitcast(FP8X4),
+                    scales=x_scales[:, steps, :].rearrange("p t c -> p (t c)"),
+                    in_=grouped_flat,
+                )
+            p_mean.append(mean_over_time(phi_q, phi_bias, x_codes, x_scales, "p", g))
+            th_mean.append(mean_over_time(theta_q, theta_bias, x_codes, x_scales, "th", g))
+
+        kappa_codes, kappa_scales = quantise_weight(kappa_raw, "kappa")
+        lam_bias = keep.tile([P, PACK], F32)
+        nc.vector.tensor_scalar_mul(out=lam_bias[:], in0=kappa_bias[:], scalar1=lam_col[:, 0:1])
+        a_plus = keep.tile([P, PACK, JOINTS * JOINTS], F32)
+        for m in range(PACK):
+            nc.scalar.activation(
+                out=a_plus[:, m, :], in_=a_bf16[:, m, :], func=ACT.Identity, bias=lam_bias[:, m : m + 1], scale=1.0
+            )
+
+        for b in range(BATCH):
+            g, first = b // GROUP, (b % GROUP) * JOINTS
+            out_b = out[b].rearrange("(q m) u v -> q m (u v)", m=PACK)
+            for half in range(2):
+                shape = [P, HALF_JOINTS, JOINTS, PACK]
+                u0 = first + half * HALF_JOINTS
+                diff = work.tile(shape, F32)
+                nc.vector.tensor_tensor(
+                    out=diff[:],
+                    in0=p_mean[g][:, u0 : u0 + HALF_JOINTS, :].unsqueeze(2).to_broadcast(shape),
+                    in1=th_mean[g][:, first : first + JOINTS, :].unsqueeze(1).to_broadcast(shape),
+                    op=ALU.subtract,
+                )
+                f_bf16 = work.tile([P, PAIRS * PACK], BF16, align_bytes=64)
+                nc.scalar.activation(out=f_bf16[:], in_=diff[:].rearrange("p u v m -> p (u v m)"), func=ACT.Tanh)
+                f_codes = work.tile([P, PAIRS], U32, align_bytes=64)
+                f_scales = work.tile([P, PAIRS], U8, align_bytes=64)
+                nc.vector.quantize_mx(out=f_codes[:].bitcast(FP8X4), scales=f_scales[:], in_=f_bf16[:])
+
+                pairs = slice(half * PAIRS, (half + 1) * PAIRS)
+                result = work.tile([P, PACK, PAIRS], F32)
+                for m in range(PACK):
+                    acc = ps_acc.tile([P, PAIRS], F32)
+                    nc.tensor.matmul_mx(
+                        out=acc[:],
+                        lhsT=kappa_codes[:, m, :].bitcast(FP8X4),
+                        lhsT_scale=kappa_scales[:, m, :],
+                        rhs=f_codes[:].bitcast(FP8X4),
+                        rhs_scale=f_scales[:],
+                        start=True,
+                        stop=True,
+                    )
+                    nc.vector.scalar_tensor_tensor(
+                        out=result[:, m, :],
+                        in0=acc[:],
+                        scalar=lam_col[:, 0:1],
+                        in1=a_plus[:, m, pairs],
+                        op0=ALU.mult,
+                        op1=ALU.add,
+                    )
+                nc.sync.dma_start(out=out_b[:, :, pairs], in_=result[:])

@@ -22,6 +22,7 @@ ROWS_STEPS = P // JOINTS
 HALF_STEPS = 2 * ROWS_STEPS
 HALF_JOINTS = JOINTS // 2
 PAIRS = HALF_JOINTS * JOINTS
+GPSIMD_JOINTS = 8
 
 FLOPS = 2 * BATCH * STEPS * JOINTS * WIDTH * 2 * WIDTH + 2 * BATCH * JOINTS * JOINTS * WIDTH * WIDTH
 
@@ -164,15 +165,17 @@ def tile_attgcn_pa_t_kernel(
             g, first = b // GROUP, (b % GROUP) * JOINTS
             out_b = out[b].rearrange("(q m) u v -> q m (u v)", m=PACK)
             for half in range(2):
-                shape = [P, HALF_JOINTS, JOINTS, PACK]
                 u0 = first + half * HALF_JOINTS
-                diff = work.tile(shape, F32)
-                nc.vector.tensor_tensor(
-                    out=diff[:],
-                    in0=p_mean[g][:, u0 : u0 + HALF_JOINTS, :].unsqueeze(2).to_broadcast(shape),
-                    in1=th_mean[g][:, first : first + JOINTS, :].unsqueeze(1).to_broadcast(shape),
-                    op=ALU.subtract,
-                )
+                diff = work.tile([P, HALF_JOINTS, JOINTS, PACK], F32)
+                split = HALF_JOINTS - GPSIMD_JOINTS
+                for engine, lo, hi in ((nc.vector, 0, split), (nc.gpsimd, split, HALF_JOINTS)):
+                    shape = [P, hi - lo, JOINTS, PACK]
+                    engine.tensor_tensor(
+                        out=diff[:, lo:hi],
+                        in0=p_mean[g][:, u0 + lo : u0 + hi, :].unsqueeze(2).to_broadcast(shape),
+                        in1=th_mean[g][:, first : first + JOINTS, :].unsqueeze(1).to_broadcast(shape),
+                        op=ALU.subtract,
+                    )
                 f_bf16 = work.tile([P, PAIRS * PACK], BF16, align_bytes=64)
                 nc.scalar.activation(out=f_bf16[:], in_=diff[:].rearrange("p u v m -> p (u v m)"), func=ACT.Tanh)
                 f_codes = work.tile([P, PAIRS], U32, align_bytes=64)

@@ -38,7 +38,7 @@ def tile_attgcn_pa_t_kernel(
         work = stack.enter_context(tc.tile_pool(name="work", bufs=3))
         ps_xt = stack.enter_context(tc.psum_pool(name="ps_xt", bufs=2))
         ps_sum = stack.enter_context(tc.psum_pool(name="ps_sum", bufs=1))
-        ps_acc = stack.enter_context(tc.psum_pool(name="ps_acc", bufs=4))
+        ps_acc = stack.enter_context(tc.psum_pool(name="ps_acc", bufs=3))
 
         def load_weight(w, label):
             raw = keep.tile([P, PACK, WIDTH], BF16, name="%s_raw" % label)
@@ -98,9 +98,9 @@ def tile_attgcn_pa_t_kernel(
         phi_q = quantise_weight(phi_raw, "phi")
         theta_q = quantise_weight(theta_raw, "theta")
 
-        def mean_over_time(weight_q, bias, x_codes, x_scales, kind, g):
+        def sum_over_time(weight_q, x_codes, x_scales, kind, bufs):
             w_codes, w_scales = weight_q
-            sums = ps_sum.tile([P, PACK, P], F32, tag="%s_sums" % kind)
+            sums = ps_sum.tile([P, PACK, P], F32, tag="%s_sums" % kind, bufs=bufs)
             for m in range(PACK):
                 for t in range(STEPS):
                     nc.tensor.matmul_mx(
@@ -112,18 +112,13 @@ def tile_attgcn_pa_t_kernel(
                         start=(t == 0),
                         stop=(t == STEPS - 1),
                     )
-            mean = keep.tile([P, P, PACK], F32, name="%s_mean%d" % (kind, g))
-            nc.vector.scalar_tensor_tensor(
-                out=mean[:],
-                in0=sums[:].rearrange("p m c -> p c m"),
-                scalar=1.0 / STEPS,
-                in1=bias[:].unsqueeze(1).to_broadcast([P, P, PACK]),
-                op0=ALU.mult,
-                op1=ALU.add,
-            )
-            return mean
+            return sums[:].rearrange("p m c -> p c m")
 
-        p_mean, th_mean = [], []
+        bias16 = keep.tile([P, PACK], F32)
+        nc.vector.tensor_sub(out=bias16[:], in0=theta_bias[:], in1=phi_bias[:])
+        nc.vector.tensor_scalar_mul(out=bias16[:], in0=bias16[:], scalar1=float(STEPS))
+
+        p_psum, p_sbuf, th_sbuf = [], [], []
         for g in range(N_GROUPS):
             x_codes = keep.tile([P, STEPS, P], U32, align_bytes=64, name="x_codes%d" % g)
             x_scales = keep.tile([P, STEPS, P], U8, align_bytes=64, name="x_scales%d" % g)
@@ -149,8 +144,17 @@ def tile_attgcn_pa_t_kernel(
                     scales=x_scales[:, steps, :].rearrange("p t c -> p (t c)"),
                     in_=grouped_flat,
                 )
-            p_mean.append(mean_over_time(phi_q, phi_bias, x_codes, x_scales, "p", g))
-            th_mean.append(mean_over_time(theta_q, theta_bias, x_codes, x_scales, "th", g))
+            p_sums = sum_over_time(phi_q, x_codes, x_scales, "p", N_GROUPS)
+            p_copy = keep.tile([P, P, PACK], F32, name="p_copy%d" % g)
+            nc.vector.tensor_copy(out=p_copy[:], in_=p_sums)
+            th_sums = sum_over_time(theta_q, x_codes, x_scales, "th", 1)
+            th_shifted = keep.tile([P, P, PACK], F32, name="th_shifted%d" % g)
+            nc.vector.tensor_tensor(
+                out=th_shifted[:], in0=th_sums, in1=bias16[:].unsqueeze(1).to_broadcast([P, P, PACK]), op=ALU.add
+            )
+            p_psum.append(p_sums)
+            p_sbuf.append(p_copy)
+            th_sbuf.append(th_shifted)
 
         kappa_codes, kappa_scales = quantise_weight(kappa_raw, "kappa")
         lam_bias = keep.tile([P, PACK], F32)
@@ -168,16 +172,19 @@ def tile_attgcn_pa_t_kernel(
                 u0 = first + half * HALF_JOINTS
                 diff = work.tile([P, HALF_JOINTS, JOINTS, PACK], F32)
                 split = HALF_JOINTS - GPSIMD_JOINTS
-                for engine, lo, hi in ((nc.vector, 0, split), (nc.gpsimd, split, HALF_JOINTS)):
+                for engine, p_sums, lo, hi in (
+                    (nc.vector, p_psum[g], 0, split),
+                    (nc.gpsimd, p_sbuf[g][:], split, HALF_JOINTS),
+                ):
                     shape = [P, hi - lo, JOINTS, PACK]
                     engine.tensor_tensor(
                         out=diff[:, lo:hi],
-                        in0=p_mean[g][:, u0 + lo : u0 + hi, :].unsqueeze(2).to_broadcast(shape),
-                        in1=th_mean[g][:, first : first + JOINTS, :].unsqueeze(1).to_broadcast(shape),
+                        in0=p_sums[:, u0 + lo : u0 + hi, :].unsqueeze(2).to_broadcast(shape),
+                        in1=th_sbuf[g][:, first : first + JOINTS, :].unsqueeze(1).to_broadcast(shape),
                         op=ALU.subtract,
                     )
                 f_bf16 = work.tile([P, PAIRS * PACK], BF16, align_bytes=64)
-                nc.scalar.activation(out=f_bf16[:], in_=diff[:].rearrange("p u v m -> p (u v m)"), func=ACT.Tanh)
+                nc.scalar.activation(out=f_bf16[:], in_=diff[:].rearrange("p u v m -> p (u v m)"), func=ACT.Tanh, scale=1.0 / STEPS)
                 f_codes = work.tile([P, PAIRS], U32, align_bytes=64)
                 f_scales = work.tile([P, PAIRS], U8, align_bytes=64)
                 nc.vector.quantize_mx(out=f_codes[:].bitcast(FP8X4), scales=f_scales[:], in_=f_bf16[:])

@@ -22,7 +22,7 @@ ROWS_STEPS = P // JOINTS
 HALF_STEPS = 2 * ROWS_STEPS
 HALF_JOINTS = JOINTS // 2
 PAIRS = HALF_JOINTS * JOINTS
-GPSIMD_JOINTS = 8
+GPSIMD_JOINTS = 6
 
 FLOPS = 2 * BATCH * STEPS * JOINTS * WIDTH * 2 * WIDTH + 2 * BATCH * JOINTS * JOINTS * WIDTH * WIDTH
 

@@ -22,7 +22,8 @@ ROWS_STEPS = P // JOINTS
 HALF_STEPS = 2 * ROWS_STEPS
 HALF_JOINTS = JOINTS // 2
 PAIRS = HALF_JOINTS * JOINTS
-GPSIMD_JOINTS = 6
+GPSIMD_JOINTS = 8
+GPSIMD_PIECE = 4
 
 FLOPS = 2 * BATCH * STEPS * JOINTS * WIDTH * 2 * WIDTH + 2 * BATCH * JOINTS * JOINTS * WIDTH * WIDTH
 
@@ -35,10 +36,10 @@ def tile_attgcn_pa_t_kernel(
         keep = stack.enter_context(tc.tile_pool(name="keep", bufs=1))
         x_pool = stack.enter_context(tc.tile_pool(name="x_rows", bufs=N_GROUPS * STEPS // ROWS_STEPS))
         stage = stack.enter_context(tc.tile_pool(name="stage", bufs=2))
-        work = stack.enter_context(tc.tile_pool(name="work", bufs=3))
-        ps_xt = stack.enter_context(tc.psum_pool(name="ps_xt", bufs=2))
-        ps_sum = stack.enter_context(tc.psum_pool(name="ps_sum", bufs=1))
-        ps_acc = stack.enter_context(tc.psum_pool(name="ps_acc", bufs=3))
+        work = stack.enter_context(tc.tile_pool(name="work", bufs=4))
+        results = stack.enter_context(tc.tile_pool(name="results", bufs=4 * PACK))
+        ps_keep = stack.enter_context(tc.psum_pool(name="ps_keep", bufs=N_GROUPS))
+        ps_bank = stack.enter_context(tc.psum_pool(name="ps_bank", bufs=8 - N_GROUPS))
 
         def load_weight(w, label):
             raw = keep.tile([P, PACK, WIDTH], BF16, name="%s_raw" % label)
@@ -98,9 +99,9 @@ def tile_attgcn_pa_t_kernel(
         phi_q = quantise_weight(phi_raw, "phi")
         theta_q = quantise_weight(theta_raw, "theta")
 
-        def sum_over_time(weight_q, x_codes, x_scales, kind, bufs):
+        def sum_over_time(weight_q, x_codes, x_scales, pool, tag):
             w_codes, w_scales = weight_q
-            sums = ps_sum.tile([P, PACK, P], F32, tag="%s_sums" % kind, bufs=bufs)
+            sums = pool.tile([P, PACK, P], F32, tag=tag)
             for m in range(PACK):
                 for t in range(STEPS):
                     nc.tensor.matmul_mx(
@@ -129,7 +130,7 @@ def tile_attgcn_pa_t_kernel(
                     "p (t b v i) -> p t b v i", t=HALF_STEPS, b=GROUP, v=JOINTS
                 )
                 for b in range(GROUP):
-                    xt = ps_xt.tile([P, 2, 2, P], F32)
+                    xt = ps_bank.tile([P, 2, 2, P], F32, tag="bank")
                     for s in range(2):
                         words = x_rows[(g, 2 * h + s)][:, b, :].bitcast(F32).rearrange("p (w i) -> p i w", i=2)
                         for i in range(2):
@@ -144,10 +145,10 @@ def tile_attgcn_pa_t_kernel(
                     scales=x_scales[:, steps, :].rearrange("p t c -> p (t c)"),
                     in_=grouped_flat,
                 )
-            p_sums = sum_over_time(phi_q, x_codes, x_scales, "p", N_GROUPS)
+            p_sums = sum_over_time(phi_q, x_codes, x_scales, ps_keep, "p_sums")
             p_copy = keep.tile([P, P, PACK], F32, name="p_copy%d" % g)
             nc.vector.tensor_copy(out=p_copy[:], in_=p_sums)
-            th_sums = sum_over_time(theta_q, x_codes, x_scales, "th", 1)
+            th_sums = sum_over_time(theta_q, x_codes, x_scales, ps_bank, "bank")
             th_shifted = keep.tile([P, P, PACK], F32, name="th_shifted%d" % g)
             nc.vector.tensor_tensor(
                 out=th_shifted[:], in0=th_sums, in1=bias16[:].unsqueeze(1).to_broadcast([P, P, PACK]), op=ALU.add
@@ -165,49 +166,73 @@ def tile_attgcn_pa_t_kernel(
                 out=a_plus[:, m, :], in_=a_bf16[:, m, :], func=ACT.Identity, bias=lam_bias[:, m : m + 1], scale=1.0
             )
 
-        for b in range(BATCH):
+        def differences(unit):
+            b, half = unit // 2, unit % 2
             g, first = b // GROUP, (b % GROUP) * JOINTS
-            out_b = out[b].rearrange("(q m) u v -> q m (u v)", m=PACK)
-            for half in range(2):
-                u0 = first + half * HALF_JOINTS
-                diff = work.tile([P, HALF_JOINTS, JOINTS, PACK], F32)
-                split = HALF_JOINTS - GPSIMD_JOINTS
-                for engine, p_sums, lo, hi in (
-                    (nc.vector, p_psum[g], 0, split),
-                    (nc.gpsimd, p_sbuf[g][:], split, HALF_JOINTS),
-                ):
-                    shape = [P, hi - lo, JOINTS, PACK]
-                    engine.tensor_tensor(
-                        out=diff[:, lo:hi],
-                        in0=p_sums[:, u0 + lo : u0 + hi, :].unsqueeze(2).to_broadcast(shape),
-                        in1=th_sbuf[g][:, first : first + JOINTS, :].unsqueeze(1).to_broadcast(shape),
-                        op=ALU.subtract,
-                    )
-                f_bf16 = work.tile([P, PAIRS * PACK], BF16, align_bytes=64)
-                nc.scalar.activation(out=f_bf16[:], in_=diff[:].rearrange("p u v m -> p (u v m)"), func=ACT.Tanh, scale=1.0 / STEPS)
-                f_codes = work.tile([P, PAIRS], U32, align_bytes=64)
-                f_scales = work.tile([P, PAIRS], U8, align_bytes=64)
-                nc.vector.quantize_mx(out=f_codes[:].bitcast(FP8X4), scales=f_scales[:], in_=f_bf16[:])
+            u0 = first + half * HALF_JOINTS
+            diff = work.tile([P, HALF_JOINTS, JOINTS, PACK], F32)
 
-                pairs = slice(half * PAIRS, (half + 1) * PAIRS)
-                result = work.tile([P, PACK, PAIRS], F32)
-                for m in range(PACK):
-                    acc = ps_acc.tile([P, PAIRS], F32)
-                    nc.tensor.matmul_mx(
-                        out=acc[:],
-                        lhsT=kappa_codes[:, m, :].bitcast(FP8X4),
-                        lhsT_scale=kappa_scales[:, m, :],
-                        rhs=f_codes[:].bitcast(FP8X4),
-                        rhs_scale=f_scales[:],
-                        start=True,
-                        stop=True,
-                    )
-                    nc.vector.scalar_tensor_tensor(
-                        out=result[:, m, :],
-                        in0=acc[:],
-                        scalar=lam_col[:, 0:1],
-                        in1=a_plus[:, m, pairs],
-                        op0=ALU.mult,
-                        op1=ALU.add,
-                    )
-                nc.sync.dma_start(out=out_b[:, :, pairs], in_=result[:])
+            def subtract(engine, p_sums, lo, hi):
+                shape = [P, hi - lo, JOINTS, PACK]
+                engine.tensor_tensor(
+                    out=diff[:, lo:hi],
+                    in0=p_sums[:, u0 + lo : u0 + hi, :].unsqueeze(2).to_broadcast(shape),
+                    in1=th_sbuf[g][:, first : first + JOINTS, :].unsqueeze(1).to_broadcast(shape),
+                    op=ALU.subtract,
+                )
+
+            split = HALF_JOINTS - GPSIMD_JOINTS
+            subtract(nc.vector, p_psum[g], 0, split)
+            for lo in range(split, HALF_JOINTS, GPSIMD_PIECE):
+                subtract(nc.gpsimd, p_sbuf[g][:], lo, lo + GPSIMD_PIECE)
+            return diff
+
+        def squash(diff):
+            f_bf16 = work.tile([P, PAIRS * PACK], BF16, align_bytes=64)
+            nc.scalar.activation(
+                out=f_bf16[:], in_=diff[:].rearrange("p u v m -> p (u v m)"), func=ACT.Tanh, scale=1.0 / STEPS
+            )
+            return f_bf16
+
+        def quantise(f_bf16):
+            f_codes = work.tile([P, PAIRS], U32, align_bytes=64)
+            f_scales = work.tile([P, PAIRS], U8, align_bytes=64)
+            nc.vector.quantize_mx(out=f_codes[:].bitcast(FP8X4), scales=f_scales[:], in_=f_bf16[:])
+            return f_codes, f_scales
+
+        def multiply_and_store(unit, f_codes, f_scales):
+            b, half = unit // 2, unit % 2
+            pairs = slice(half * PAIRS, (half + 1) * PAIRS)
+            out_b = out[b].rearrange("(q m) u v -> q m (u v)", m=PACK)
+            for m in range(PACK):
+                acc = ps_bank.tile([P, PAIRS], F32, tag="bank")
+                nc.tensor.matmul_mx(
+                    out=acc[:],
+                    lhsT=kappa_codes[:, m, :].bitcast(FP8X4),
+                    lhsT_scale=kappa_scales[:, m, :],
+                    rhs=f_codes[:].bitcast(FP8X4),
+                    rhs_scale=f_scales[:],
+                    start=True,
+                    stop=True,
+                )
+                result = results.tile([P, PAIRS], F32)
+                nc.vector.scalar_tensor_tensor(
+                    out=result[:],
+                    in0=acc[:],
+                    scalar=lam_col[:, 0:1],
+                    in1=a_plus[:, m, pairs],
+                    op0=ALU.mult,
+                    op1=ALU.add,
+                )
+                nc.sync.dma_start(out=out_b[:, m, pairs], in_=result[:])
+
+        n_units = 2 * BATCH
+        diffs = [differences(0), differences(1)]
+        squashed = [squash(diffs[0])]
+        for unit in range(n_units):
+            f_codes, f_scales = quantise(squashed[unit])
+            if unit + 2 < n_units:
+                diffs.append(differences(unit + 2))
+            if unit + 1 < n_units:
+                squashed.append(squash(diffs[unit + 1]))
+            multiply_and_store(unit, f_codes, f_scales)

@@ -10,20 +10,37 @@ U8 = mybir.dt.uint8
 FP8X4 = mybir.dt.float8_e4m3fn_x4
 ALU = mybir.AluOpType
 ACT = mybir.ActivationFunctionType
+ENGINE = mybir.EngineType
 
 BATCH, STEPS, JOINTS, WIDTH = 8, 16, 32, 512
 P = 128
 PACK = 4
 assert P * PACK == WIDTH
 
-GROUP = P // JOINTS
+GROUP = 2
 N_GROUPS = BATCH // GROUP
+COLS = GROUP * JOINTS
+PASS_STEPS = P // COLS
+PASSES = STEPS // PASS_STEPS
 ROWS_STEPS = P // JOINTS
+ROWS_TILES = STEPS // ROWS_STEPS
 HALF_STEPS = 2 * ROWS_STEPS
-HALF_JOINTS = JOINTS // 2
-PAIRS = HALF_JOINTS * JOINTS
-GPSIMD_JOINTS = 8
-GPSIMD_PIECE = 4
+
+QUAD = 4
+QUAD_PAIRS = QUAD * JOINTS
+QUAD_WIDTH = QUAD_PAIRS * PACK
+UNIT_QUADS = 4
+PAIRS = UNIT_QUADS * QUAD_PAIRS
+BATCH_QUADS = JOINTS // QUAD
+N_QUADS = BATCH * BATCH_QUADS
+N_UNITS = N_QUADS // UNIT_QUADS
+OCTET = 8
+OCTETS = JOINTS // OCTET
+TERMS = 3
+P_ROW = TERMS * JOINTS
+
+TENSOR_BATCHES = (3, 4, 5, 7)
+VECTOR_QUADS = (0, 1, 2, 4, 5, 11, 15, 19, 23)
 
 FLOPS = 2 * BATCH * STEPS * JOINTS * WIDTH * 2 * WIDTH + 2 * BATCH * JOINTS * JOINTS * WIDTH * WIDTH
 
@@ -34,27 +51,32 @@ def tile_attgcn_pa_t_kernel(
     nc = tc.nc
     with ExitStack() as stack:
         keep = stack.enter_context(tc.tile_pool(name="keep", bufs=1))
-        x_pool = stack.enter_context(tc.tile_pool(name="x_rows", bufs=N_GROUPS * STEPS // ROWS_STEPS))
+        x_pool = stack.enter_context(tc.tile_pool(name="x_rows", bufs=N_GROUPS * ROWS_TILES))
         stage = stack.enter_context(tc.tile_pool(name="stage", bufs=2))
-        work = stack.enter_context(tc.tile_pool(name="work", bufs=4))
-        results = stack.enter_context(tc.tile_pool(name="results", bufs=4 * PACK))
-        ps_keep = stack.enter_context(tc.psum_pool(name="ps_keep", bufs=N_GROUPS))
-        ps_bank = stack.enter_context(tc.psum_pool(name="ps_bank", bufs=8 - N_GROUPS))
+        split = stack.enter_context(tc.tile_pool(name="split", bufs=2))
+        quads = stack.enter_context(tc.tile_pool(name="quads", bufs=6))
+        work = stack.enter_context(tc.tile_pool(name="work", bufs=3))
+        results = stack.enter_context(tc.tile_pool(name="results", bufs=12))
+        ps_out = stack.enter_context(tc.psum_pool(name="ps_out", bufs=3))
+        ps_bank = stack.enter_context(tc.psum_pool(name="ps_bank", bufs=5))
 
         def load_weight(w, label):
             raw = keep.tile([P, PACK, WIDTH], BF16, name="%s_raw" % label)
             nc.sync.dma_start(out=raw[:], in_=w.rearrange("(p j) c -> p j c", j=PACK))
             return raw
 
-        def load_x(g, s):
-            rows = x_pool.tile([P, GROUP, WIDTH], BF16)
-            nc.sync.dma_start(
-                out=rows[:],
-                in_=x[g * GROUP : (g + 1) * GROUP, s * ROWS_STEPS : (s + 1) * ROWS_STEPS].rearrange(
-                    "b t v f -> (t v) b f"
-                ),
-            )
-            return rows
+        def load_x(g):
+            tiles = []
+            for s in range(ROWS_TILES):
+                rows = x_pool.tile([P, GROUP, WIDTH], BF16)
+                nc.sync.dma_start(
+                    out=rows[:],
+                    in_=x[g * GROUP : (g + 1) * GROUP, s * ROWS_STEPS : (s + 1) * ROWS_STEPS].rearrange(
+                        "b t v f -> (t v) b f"
+                    ),
+                )
+                tiles.append(rows)
+            return tiles
 
         def load_per_channel(vec, label):
             narrow = keep.tile([P, PACK], BF16, name="%s_bf16" % label)
@@ -65,16 +87,17 @@ def tile_attgcn_pa_t_kernel(
 
         ident = keep.tile([P, P], F32)
         make_identity(nc, ident[:])
+        ident_bf16 = keep.tile([P, P], BF16)
+        nc.gpsimd.tensor_copy(out=ident_bf16[:], in_=ident[:])
 
-        n_tiles = STEPS // ROWS_STEPS
         phi_raw = load_weight(phi_w, "phi")
-        x_rows = {(0, s): load_x(0, s) for s in range(n_tiles)}
+        x_rows = [load_x(0)]
         theta_raw = load_weight(theta_w, "theta")
-        for s in range(n_tiles):
-            x_rows[(1, s)] = load_x(1, s)
         kappa_raw = load_weight(kappa_w, "kappa")
         a_bf16 = keep.tile([P, PACK, JOINTS * JOINTS], BF16)
         nc.sync.dma_start(out=a_bf16[:], in_=A.rearrange("(q m) u v -> q m (u v)", m=PACK))
+        for g in range(1, N_GROUPS):
+            x_rows.append(load_x(g))
 
         phi_bias = load_per_channel(phi_b, "phi_b")
         theta_bias = load_per_channel(theta_b, "theta_b")
@@ -83,9 +106,38 @@ def tile_attgcn_pa_t_kernel(
         nc.scalar.dma_start(out=lam_bf16[:], in_=lam.partition_broadcast(P))
         lam_col = keep.tile([P, 1], F32)
         nc.vector.tensor_copy(out=lam_col[:], in_=lam_bf16[:])
+        bias16 = keep.tile([P, PACK], F32)
+        nc.vector.tensor_sub(out=bias16[:], in0=theta_bias[:], in1=phi_bias[:])
+        nc.vector.tensor_scalar_mul(out=bias16[:], in0=bias16[:], scalar1=float(STEPS))
+        lam_bias = keep.tile([P, PACK], F32)
+        nc.vector.tensor_scalar_mul(out=lam_bias[:], in0=kappa_bias[:], scalar1=lam_col[:, 0:1])
+
+        th_rows = keep.tile([P, JOINTS], F32)
+        p_rows = keep.tile([P, OCTET], F32)
+        for rows, first, width in ((th_rows, 0, JOINTS), (p_rows, P_ROW, OCTET)):
+            nc.gpsimd.tensor_tensor(
+                out=rows[:], in0=ident[:, first : first + width], in1=ident[:, first + width : first + 2 * width], op=ALU.add
+            )
+            nc.gpsimd.tensor_tensor(
+                out=rows[:], in0=rows[:], in1=ident[:, first + 2 * width : first + 3 * width], op=ALU.add
+            )
+        select = keep.tile([P, OCTET, JOINTS], BF16)
+        nc.gpsimd.tensor_tensor(
+            out=select[:],
+            in0=p_rows[:].unsqueeze(2).to_broadcast([P, OCTET, JOINTS]),
+            in1=th_rows[:].unsqueeze(1).to_broadcast([P, OCTET, JOINTS]),
+            op=ALU.subtract,
+        )
+        terms_tiles = []
+        for i in range(2):
+            terms = keep.tile([P, OCTETS, PACK, P], BF16, name="terms%d" % i)
+            nc.gpsimd.memset(terms[:, :, :, P_ROW + TERMS * OCTET :], 0.0)
+            terms_tiles.append(terms)
+
+        stack.enter_context(tc.manual_schedule(engines={ENGINE.PE, ENGINE.DVE, ENGINE.Activation, ENGINE.Pool}))
 
         def quantise_weight(raw, label):
-            grouped = stage.tile([P, PACK, P, PACK], BF16, align_bytes=64, tag="w_grouped")
+            grouped = stage.tile([P, PACK, P, PACK], BF16, align_bytes=64, tag="grouped")
             nc.vector.tensor_copy(out=grouped[:], in_=raw[:].rearrange("p j (q m) -> p m q j", m=PACK))
             codes = keep.tile([P, PACK, P], U32, align_bytes=64, name="%s_codes" % label)
             scales = keep.tile([P, PACK, P], U8, align_bytes=64, name="%s_scales" % label)
@@ -96,143 +148,287 @@ def tile_attgcn_pa_t_kernel(
             )
             return codes, scales
 
-        phi_q = quantise_weight(phi_raw, "phi")
-        theta_q = quantise_weight(theta_raw, "theta")
+        weight_q = {"phi": quantise_weight(phi_raw, "phi")}
 
-        def sum_over_time(weight_q, x_codes, x_scales, pool, tag):
-            w_codes, w_scales = weight_q
-            sums = pool.tile([P, PACK, P], F32, tag=tag)
-            for m in range(PACK):
-                for t in range(STEPS):
-                    nc.tensor.matmul_mx(
-                        out=sums[:, m, :],
-                        lhsT=w_codes[:, m, :].bitcast(FP8X4),
-                        lhsT_scale=w_scales[:, m, :],
-                        rhs=x_codes[:, t, :].bitcast(FP8X4),
-                        rhs_scale=x_scales[:, t, :],
-                        start=(t == 0),
-                        stop=(t == STEPS - 1),
-                    )
-            return sums[:].rearrange("p m c -> p c m")
-
-        bias16 = keep.tile([P, PACK], F32)
-        nc.vector.tensor_sub(out=bias16[:], in0=theta_bias[:], in1=phi_bias[:])
-        nc.vector.tensor_scalar_mul(out=bias16[:], in0=bias16[:], scalar1=float(STEPS))
-
-        p_psum, p_sbuf, th_sbuf = [], [], []
+        p_sbuf, th_sbuf = [], []
         for g in range(N_GROUPS):
-            x_codes = keep.tile([P, STEPS, P], U32, align_bytes=64, name="x_codes%d" % g)
-            x_scales = keep.tile([P, STEPS, P], U8, align_bytes=64, name="x_scales%d" % g)
-            for h in range(STEPS // HALF_STEPS):
-                grouped = stage.tile([P, HALF_STEPS, GROUP, JOINTS, PACK], BF16, align_bytes=64, tag="x_grouped")
-                grouped_flat = grouped[:].rearrange("p t b v j -> p (t b v j)")
-                grouped_words = grouped_flat.bitcast(F32).rearrange(
+            p_tile = keep.tile([P, COLS, PACK], F32, name="p%d" % g)
+            th_tile = keep.tile([P, COLS, PACK], F32, name="th%d" % g)
+            p_sbuf.append(p_tile)
+            th_sbuf.append(th_tile)
+
+        def stage1_pieces(g):
+            x_codes = keep.tile([P, PASSES, P], U32, align_bytes=64, name="x_codes%d" % g)
+            x_scales = keep.tile([P, PASSES, P], U8, align_bytes=64, name="x_scales%d" % g)
+            grouped_of, sums_of = {}, {}
+
+            def transpose(h, b):
+                if b == 0:
+                    grouped = stage.tile([P, HALF_STEPS, GROUP, JOINTS, PACK], BF16, align_bytes=64, tag="grouped")
+                    grouped_of[h] = grouped[:].rearrange("p t b v j -> p (t b v j)")
+                grouped_words = grouped_of[h].bitcast(F32).rearrange(
                     "p (t b v i) -> p t b v i", t=HALF_STEPS, b=GROUP, v=JOINTS
                 )
-                for b in range(GROUP):
-                    xt = ps_bank.tile([P, 2, 2, P], F32, tag="bank")
-                    for s in range(2):
-                        words = x_rows[(g, 2 * h + s)][:, b, :].bitcast(F32).rearrange("p (w i) -> p i w", i=2)
-                        for i in range(2):
-                            nc.tensor.transpose(xt[:, i, s, :], words[:, i, :], ident[:])
-                    nc.scalar.copy(
-                        out=grouped_words[:, :, b, :, :],
-                        in_=xt[:].rearrange("p i s (t v) -> p (s t) v i", v=JOINTS),
-                    )
-                steps = slice(h * HALF_STEPS, (h + 1) * HALF_STEPS)
+                xt = ps_bank.tile([P, 2, 2, P], F32, tag="bank")
+                for s in range(2):
+                    words = x_rows[g][2 * h + s][:, b, :].bitcast(F32).rearrange("p (w i) -> p i w", i=2)
+                    for i in range(2):
+                        nc.tensor.transpose(xt[:, i, s, :], words[:, i, :], ident[:])
+                nc.scalar.copy(
+                    out=grouped_words[:, :, b, :, :],
+                    in_=xt[:].rearrange("p i s (t v) -> p (s t) v i", v=JOINTS),
+                )
+
+            def quantise_x(h):
+                half = slice(h * PASSES // 2, (h + 1) * PASSES // 2)
                 nc.vector.quantize_mx(
-                    out=x_codes[:, steps, :].rearrange("p t c -> p (t c)").bitcast(FP8X4),
-                    scales=x_scales[:, steps, :].rearrange("p t c -> p (t c)"),
-                    in_=grouped_flat,
+                    out=x_codes[:, half, :].rearrange("p t c -> p (t c)").bitcast(FP8X4),
+                    scales=x_scales[:, half, :].rearrange("p t c -> p (t c)"),
+                    in_=grouped_of[h],
                 )
-            p_sums = sum_over_time(phi_q, x_codes, x_scales, ps_keep, "p_sums")
-            p_copy = keep.tile([P, P, PACK], F32, name="p_copy%d" % g)
-            nc.vector.tensor_copy(out=p_copy[:], in_=p_sums)
-            th_sums = sum_over_time(theta_q, x_codes, x_scales, ps_bank, "bank")
-            th_shifted = keep.tile([P, P, PACK], F32, name="th_shifted%d" % g)
-            nc.vector.tensor_tensor(
-                out=th_shifted[:], in0=th_sums, in1=bias16[:].unsqueeze(1).to_broadcast([P, P, PACK]), op=ALU.add
-            )
-            p_psum.append(p_sums)
-            p_sbuf.append(p_copy)
-            th_sbuf.append(th_shifted)
 
+            def multiply(label, m):
+                w_codes, w_scales = weight_q[label]
+                if m == 0:
+                    sums = ps_bank.tile([P, PACK, P], F32, tag="bank")
+                    sums_of[label] = sums
+                for k in range(PASSES):
+                    nc.tensor.matmul_mx(
+                        out=sums_of[label][:, m, :],
+                        lhsT=w_codes[:, m, :].bitcast(FP8X4),
+                        lhsT_scale=w_scales[:, m, :],
+                        rhs=x_codes[:, k, :].bitcast(FP8X4),
+                        rhs_scale=x_scales[:, k, :],
+                        start=(k == 0),
+                        stop=(k == PASSES - 1),
+                    )
+
+            def parity(label, i):
+                return sums_of[label][:, :, i * COLS : (i + 1) * COLS].rearrange("p m c -> p c m")
+
+            def copy_odd_phi():
+                odd = split.tile([P, COLS, PACK], F32)
+                nc.scalar.copy(out=odd[:], in_=parity("phi", 1))
+                sums_of["odd phi"] = odd
+
+            def add_phi():
+                nc.vector.tensor_tensor(
+                    out=p_sbuf[g][:], in0=parity("phi", 0), in1=sums_of["odd phi"][:], op=ALU.add
+                )
+
+            def add_theta():
+                odd_th = split.tile([P, COLS, PACK], F32)
+                nc.vector.tensor_tensor(
+                    out=odd_th[:],
+                    in0=parity("theta", 1),
+                    in1=bias16[:].unsqueeze(1).to_broadcast([P, COLS, PACK]),
+                    op=ALU.add,
+                )
+                nc.vector.tensor_tensor(out=th_sbuf[g][:], in0=parity("theta", 0), in1=odd_th[:], op=ALU.add)
+
+            def calls(*functions):
+                def run():
+                    for f in functions:
+                        f()
+
+                return run
+
+            def tensor_sums(label, m):
+                return lambda: multiply(label, m)
+
+            return [
+                lambda: transpose(0, 0),
+                lambda: transpose(0, 1),
+                calls(lambda: quantise_x(0), lambda: transpose(1, 0)),
+                lambda: transpose(1, 1),
+                lambda: quantise_x(1),
+                tensor_sums("phi", 0),
+                tensor_sums("phi", 1),
+                tensor_sums("phi", 2),
+                tensor_sums("phi", 3),
+                calls(copy_odd_phi, tensor_sums("theta", 0)),
+                calls(add_phi, tensor_sums("theta", 1)),
+                tensor_sums("theta", 2),
+                tensor_sums("theta", 3),
+                add_theta,
+            ]
+
+        head = stage1_pieces(0)
+        for piece in head[:5]:
+            piece()
+        weight_q["theta"] = quantise_weight(theta_raw, "theta")
+        for piece in head[5:9]:
+            piece()
         kappa_codes, kappa_scales = quantise_weight(kappa_raw, "kappa")
-        lam_bias = keep.tile([P, PACK], F32)
-        nc.vector.tensor_scalar_mul(out=lam_bias[:], in0=kappa_bias[:], scalar1=lam_col[:, 0:1])
         a_plus = keep.tile([P, PACK, JOINTS * JOINTS], F32)
+        for piece in head[9:-1]:
+            piece()
         for m in range(PACK):
-            nc.scalar.activation(
-                out=a_plus[:, m, :], in_=a_bf16[:, m, :], func=ACT.Identity, bias=lam_bias[:, m : m + 1], scale=1.0
+            nc.vector.tensor_scalar(
+                out=a_plus[:, m, :], in0=a_bf16[:, m, :], scalar1=1.0, scalar2=lam_bias[:, m : m + 1],
+                op0=ALU.mult, op1=ALU.add,
             )
+        head[-1]()
 
-        def differences(unit):
-            b, half = unit // 2, unit % 2
+        def split_terms(b):
             g, first = b // GROUP, (b % GROUP) * JOINTS
-            u0 = first + half * HALF_JOINTS
-            diff = work.tile([P, HALF_JOINTS, JOINTS, PACK], F32)
+            terms = terms_tiles[b % 2]
+            th = th_sbuf[g][:, first : first + JOINTS, :].rearrange("p v m -> p m v")
+            p = p_sbuf[g][:, first : first + JOINTS, :].rearrange("p (o u) m -> p o m u", u=OCTET)
+            th_shape = [P, OCTETS, PACK, JOINTS]
 
-            def subtract(engine, p_sums, lo, hi):
-                shape = [P, hi - lo, JOINTS, PACK]
-                engine.tensor_tensor(
-                    out=diff[:, lo:hi],
-                    in0=p_sums[:, u0 + lo : u0 + hi, :].unsqueeze(2).to_broadcast(shape),
-                    in1=th_sbuf[g][:, first : first + JOINTS, :].unsqueeze(1).to_broadcast(shape),
-                    op=ALU.subtract,
-                )
+            def all_octets(ap):
+                return ap.unsqueeze(1).to_broadcast(th_shape)
 
-            split = HALF_JOINTS - GPSIMD_JOINTS
-            subtract(nc.vector, p_psum[g], 0, split)
-            for lo in range(split, HALF_JOINTS, GPSIMD_PIECE):
-                subtract(nc.gpsimd, p_sbuf[g][:], lo, lo + GPSIMD_PIECE)
-            return diff
+            def th_term(i):
+                return terms[:, :, :, i * JOINTS : (i + 1) * JOINTS]
 
-        def squash(diff):
-            f_bf16 = work.tile([P, PAIRS * PACK], BF16, align_bytes=64)
-            nc.scalar.activation(
-                out=f_bf16[:], in_=diff[:].rearrange("p u v m -> p (u v m)"), func=ACT.Tanh, scale=1.0 / STEPS
+            def p_term(i):
+                return terms[:, :, :, P_ROW + i * OCTET : P_ROW + (i + 1) * OCTET]
+
+            def as_bf16(out, in_):
+                nc.gpsimd.tensor_scalar(out=out, in0=in_, scalar1=1.0, scalar2=0.0, op0=ALU.mult, op1=ALU.add)
+
+            def minus(out, in0, in1):
+                nc.gpsimd.tensor_tensor(out=out, in0=in0, in1=in1, op=ALU.subtract)
+
+            th_rest = split.tile([P, PACK, JOINTS], F32)
+            p_rest = split.tile([P, OCTETS, PACK, OCTET], F32)
+            as_bf16(th_term(0), all_octets(th))
+            as_bf16(p_term(0), p)
+            minus(th_rest[:], th, terms[:, 0, :, 0:JOINTS])
+            minus(p_rest[:], p, p_term(0))
+            as_bf16(th_term(1), all_octets(th_rest[:]))
+            as_bf16(p_term(1), p_rest[:])
+            minus(th_term(2), all_octets(th_rest[:]), all_octets(terms[:, 0, :, JOINTS : 2 * JOINTS]))
+            minus(p_term(2), p_rest[:], p_term(1))
+
+        operands_of = {}
+
+        def transpose_terms(b, pair):
+            if pair == 0:
+                operands = split.tile([P, OCTETS, PACK, P], BF16)
+                operands_of[b] = operands
+            o = 2 * pair
+            bank = ps_bank.tile([P, 2, PACK, P], BF16, tag="bank")
+            for i in range(2):
+                for m in range(PACK):
+                    nc.tensor.transpose(bank[:, i, m, :], terms_tiles[b % 2][:, o + i, m, :], ident_bf16[:])
+            nc.scalar.copy(out=operands_of[b][:, o : o + 2], in_=bank[:])
+
+        differences, squashed, codes_of, acc_of = {}, {}, {}, {}
+
+        def subtract(quad, engine):
+            b = quad // BATCH_QUADS
+            g, first = b // GROUP, (b % GROUP) * JOINTS
+            u0 = first + (quad % BATCH_QUADS) * QUAD
+            diff = quads.tile([P, QUAD, JOINTS, PACK], F32)
+            shape = [P, QUAD, JOINTS, PACK]
+            engine.tensor_tensor(
+                out=diff[:],
+                in0=p_sbuf[g][:, u0 : u0 + QUAD, :].unsqueeze(2).to_broadcast(shape),
+                in1=th_sbuf[g][:, first : first + JOINTS, :].unsqueeze(1).to_broadcast(shape),
+                op=ALU.subtract,
             )
-            return f_bf16
+            differences[quad] = diff[:].rearrange("p u v m -> p (u v m)")
 
-        def quantise(f_bf16):
-            f_codes = work.tile([P, PAIRS], U32, align_bytes=64)
-            f_scales = work.tile([P, PAIRS], U8, align_bytes=64)
-            nc.vector.quantize_mx(out=f_codes[:].bitcast(FP8X4), scales=f_scales[:], in_=f_bf16[:])
-            return f_codes, f_scales
-
-        def multiply_and_store(unit, f_codes, f_scales):
-            b, half = unit // 2, unit % 2
-            pairs = slice(half * PAIRS, (half + 1) * PAIRS)
-            out_b = out[b].rearrange("(q m) u v -> q m (u v)", m=PACK)
+        def multiply_terms(quad):
+            b = quad // BATCH_QUADS
+            octet, half = divmod(quad % BATCH_QUADS, OCTET // QUAD)
+            bank = ps_bank.tile([P, PACK, QUAD_PAIRS], F32, tag="bank")
             for m in range(PACK):
-                acc = ps_bank.tile([P, PAIRS], F32, tag="bank")
-                nc.tensor.matmul_mx(
-                    out=acc[:],
-                    lhsT=kappa_codes[:, m, :].bitcast(FP8X4),
-                    lhsT_scale=kappa_scales[:, m, :],
-                    rhs=f_codes[:].bitcast(FP8X4),
-                    rhs_scale=f_scales[:],
+                nc.tensor.matmul(
+                    bank[:, m, :],
+                    lhsT=operands_of[b][:, octet, m, :],
+                    rhs=select[:, half * QUAD : (half + 1) * QUAD, :].rearrange("p u v -> p (u v)"),
                     start=True,
                     stop=True,
                 )
-                result = results.tile([P, PAIRS], F32)
-                nc.vector.scalar_tensor_tensor(
-                    out=result[:],
-                    in0=acc[:],
-                    scalar=lam_col[:, 0:1],
-                    in1=a_plus[:, m, pairs],
-                    op0=ALU.mult,
-                    op1=ALU.add,
-                )
-                nc.sync.dma_start(out=out_b[:, m, pairs], in_=result[:])
+            differences[quad] = bank[:].rearrange("p m n -> p n m")
 
-        n_units = 2 * BATCH
-        diffs = [differences(0), differences(1)]
-        squashed = [squash(diffs[0])]
-        for unit in range(n_units):
-            f_codes, f_scales = quantise(squashed[unit])
-            if unit + 2 < n_units:
-                diffs.append(differences(unit + 2))
-            if unit + 1 < n_units:
-                squashed.append(squash(diffs[unit + 1]))
-            multiply_and_store(unit, f_codes, f_scales)
+        def squash(quad):
+            unit, i = divmod(quad, UNIT_QUADS)
+            if i == 0:
+                f_bf16 = work.tile([P, PAIRS, PACK], BF16, align_bytes=64)
+                squashed[unit] = f_bf16
+            f_quad = squashed[unit][:, i * QUAD_PAIRS : (i + 1) * QUAD_PAIRS, :]
+            if quad // BATCH_QUADS not in TENSOR_BATCHES:
+                f_quad = f_quad.rearrange("p n m -> p (n m)")
+            nc.scalar.activation(out=f_quad, in_=differences[quad], func=ACT.Tanh, scale=1.0 / STEPS)
+
+        def quantise(unit):
+            f_codes = work.tile([P, PAIRS], U32, align_bytes=64)
+            f_scales = work.tile([P, PAIRS], U8, align_bytes=64)
+            nc.vector.quantize_mx(
+                out=f_codes[:].bitcast(FP8X4), scales=f_scales[:], in_=squashed[unit][:].rearrange("p n m -> p (n m)")
+            )
+            codes_of[unit] = (f_codes, f_scales)
+
+        def multiply_kappa(step):
+            unit, m = divmod(step, PACK)
+            f_codes, f_scales = codes_of[unit]
+            acc = ps_out.tile([P, PAIRS], F32)
+            nc.tensor.matmul_mx(
+                out=acc[:],
+                lhsT=kappa_codes[:, m, :].bitcast(FP8X4),
+                lhsT_scale=kappa_scales[:, m, :],
+                rhs=f_codes[:].bitcast(FP8X4),
+                rhs_scale=f_scales[:],
+                start=True,
+                stop=True,
+            )
+            acc_of[step] = acc
+
+        def finish(step):
+            unit, m = divmod(step, PACK)
+            b, half = divmod(unit, 2)
+            pairs = slice(half * PAIRS, (half + 1) * PAIRS)
+            result = results.tile([P, PAIRS], F32)
+            nc.vector.scalar_tensor_tensor(
+                out=result[:],
+                in0=acc_of[step][:],
+                scalar=lam_col[:, 0:1],
+                in1=a_plus[:, m, pairs],
+                op0=ALU.mult,
+                op1=ALU.add,
+            )
+            nc.sync.dma_start(out=out[b].rearrange("(q m) u v -> q m (u v)", m=PACK)[:, m, pairs], in_=result[:])
+
+        extra = {}
+
+        def at(step, call):
+            extra.setdefault(step, []).append(call)
+
+        for g, first_step in ((1, -9), (2, 3), (3, 20)):
+            pieces = stage1_pieces(g)
+            for i in range(len(pieces)):
+                at(first_step + i, pieces[i])
+        for b in TENSOR_BATCHES:
+            first = b * BATCH_QUADS
+            at(first - 15, lambda b=b: split_terms(b))
+            at(first - 10, lambda b=b: transpose_terms(b, 0))
+            at(first - 9, lambda b=b: transpose_terms(b, 1))
+
+        def on_tensor(quad):
+            return 0 <= quad < N_QUADS and quad // BATCH_QUADS in TENSOR_BATCHES
+
+        def on_gpsimd(quad):
+            return 0 <= quad < N_QUADS and not on_tensor(quad) and quad not in VECTOR_QUADS
+
+        for step in range(-10, N_QUADS):
+            if on_gpsimd(step + 10):
+                subtract(step + 10, nc.gpsimd)
+            if step + 7 in VECTOR_QUADS:
+                subtract(step + 7, nc.vector)
+            if (step + 2) % UNIT_QUADS == 0 and 0 <= step + 2 < N_QUADS:
+                quantise((step + 2) // UNIT_QUADS)
+            if 0 <= step + 1 < N_QUADS:
+                multiply_kappa(step + 1)
+            if on_tensor(step + 8):
+                multiply_terms(step + 8)
+            if 0 <= step + 6 < N_QUADS:
+                squash(step + 6)
+            if step >= 0:
+                finish(step)
+            for call in extra.get(step, []):
+                call()

@@ -22,9 +22,7 @@ N_GROUPS = BATCH // GROUP
 COLS = GROUP * JOINTS
 PASS_STEPS = P // COLS
 PASSES = STEPS // PASS_STEPS
-ROWS_STEPS = P // JOINTS
-ROWS_TILES = STEPS // ROWS_STEPS
-HALF_STEPS = 2 * ROWS_STEPS
+HALF_STEPS = 8
 
 QUAD = 4
 QUAD_PAIRS = QUAD * JOINTS
@@ -39,8 +37,7 @@ OCTETS = JOINTS // OCTET
 TERMS = 3
 P_ROW = TERMS * JOINTS
 
-TENSOR_BATCHES = (3, 4, 5, 7)
-VECTOR_QUADS = (0, 1, 2, 4, 5, 11, 15, 19, 23)
+TENSOR_BATCHES = (3, 5, 7)
 
 FLOPS = 2 * BATCH * STEPS * JOINTS * WIDTH * 2 * WIDTH + 2 * BATCH * JOINTS * JOINTS * WIDTH * WIDTH
 
@@ -51,31 +48,36 @@ def tile_attgcn_pa_t_kernel(
     nc = tc.nc
     with ExitStack() as stack:
         keep = stack.enter_context(tc.tile_pool(name="keep", bufs=1))
-        x_pool = stack.enter_context(tc.tile_pool(name="x_rows", bufs=N_GROUPS * ROWS_TILES))
+        x_pool = stack.enter_context(tc.tile_pool(name="x_rows", bufs=N_GROUPS * GROUP * 2))
         stage = stack.enter_context(tc.tile_pool(name="stage", bufs=2))
         split = stack.enter_context(tc.tile_pool(name="split", bufs=2))
-        quads = stack.enter_context(tc.tile_pool(name="quads", bufs=6))
-        work = stack.enter_context(tc.tile_pool(name="work", bufs=3))
+        quads = stack.enter_context(tc.tile_pool(name="quads", bufs=8))
+        work = stack.enter_context(tc.tile_pool(name="work", bufs=4))
         results = stack.enter_context(tc.tile_pool(name="results", bufs=12))
+        ps_keep = stack.enter_context(tc.psum_pool(name="ps_keep", bufs=1))
         ps_out = stack.enter_context(tc.psum_pool(name="ps_out", bufs=3))
-        ps_bank = stack.enter_context(tc.psum_pool(name="ps_bank", bufs=5))
+        ps_bank = stack.enter_context(tc.psum_pool(name="ps_bank", bufs=4))
 
-        def load_weight(w, label):
+        def load_weight(w, label, halves):
             raw = keep.tile([P, PACK, WIDTH], BF16, name="%s_raw" % label)
-            nc.sync.dma_start(out=raw[:], in_=w.rearrange("(p j) c -> p j c", j=PACK))
+            nc.sync.dma_start(
+                out=raw[:].rearrange("p (i e) c -> p i e c", i=halves),
+                in_=w.rearrange("(i p e) c -> p i e c", i=halves, p=P),
+            )
             return raw
 
         def load_x(g):
-            tiles = []
-            for s in range(ROWS_TILES):
-                rows = x_pool.tile([P, GROUP, WIDTH], BF16)
-                nc.sync.dma_start(
-                    out=rows[:],
-                    in_=x[g * GROUP : (g + 1) * GROUP, s * ROWS_STEPS : (s + 1) * ROWS_STEPS].rearrange(
-                        "b t v f -> (t v) b f"
-                    ),
-                )
-                tiles.append(rows)
+            tiles = {}
+            for h in range(STEPS // HALF_STEPS):
+                for b in range(GROUP):
+                    rows = x_pool.tile([P, 2, WIDTH], BF16)
+                    nc.sync.dma_start(
+                        out=rows[:],
+                        in_=x[g * GROUP + b, h * HALF_STEPS : (h + 1) * HALF_STEPS].rearrange(
+                            "t (w e) f -> (t w) e f", e=2
+                        ),
+                    )
+                    tiles[h, b] = rows
             return tiles
 
         def load_per_channel(vec, label):
@@ -90,13 +92,14 @@ def tile_attgcn_pa_t_kernel(
         ident_bf16 = keep.tile([P, P], BF16)
         nc.gpsimd.tensor_copy(out=ident_bf16[:], in_=ident[:])
 
-        phi_raw = load_weight(phi_w, "phi")
+        phi_raw = load_weight(phi_w, "phi", 2)
         x_rows = [load_x(0)]
-        theta_raw = load_weight(theta_w, "theta")
-        kappa_raw = load_weight(kappa_w, "kappa")
+        theta_raw = load_weight(theta_w, "theta", 2)
+        kappa_raw = load_weight(kappa_w, "kappa", 1)
+        x_rows.append(load_x(1))
         a_bf16 = keep.tile([P, PACK, JOINTS * JOINTS], BF16)
         nc.sync.dma_start(out=a_bf16[:], in_=A.rearrange("(q m) u v -> q m (u v)", m=PACK))
-        for g in range(1, N_GROUPS):
+        for g in range(2, N_GROUPS):
             x_rows.append(load_x(g))
 
         phi_bias = load_per_channel(phi_b, "phi_b")
@@ -167,16 +170,16 @@ def tile_attgcn_pa_t_kernel(
                     grouped = stage.tile([P, HALF_STEPS, GROUP, JOINTS, PACK], BF16, align_bytes=64, tag="grouped")
                     grouped_of[h] = grouped[:].rearrange("p t b v j -> p (t b v j)")
                 grouped_words = grouped_of[h].bitcast(F32).rearrange(
-                    "p (t b v i) -> p t b v i", t=HALF_STEPS, b=GROUP, v=JOINTS
+                    "p (t b w k) -> p t b w k", t=HALF_STEPS, b=GROUP, w=JOINTS // 2
                 )
                 xt = ps_bank.tile([P, 2, 2, P], F32, tag="bank")
-                for s in range(2):
-                    words = x_rows[g][2 * h + s][:, b, :].bitcast(F32).rearrange("p (w i) -> p i w", i=2)
+                for e in range(2):
+                    words = x_rows[g][h, b][:, e, :].bitcast(F32).rearrange("p (i w) -> p i w", i=2)
                     for i in range(2):
-                        nc.tensor.transpose(xt[:, i, s, :], words[:, i, :], ident[:])
+                        nc.tensor.transpose(xt[:, i, e, :], words[:, i, :], ident[:])
                 nc.scalar.copy(
-                    out=grouped_words[:, :, b, :, :],
-                    in_=xt[:].rearrange("p i s (t v) -> p (s t) v i", v=JOINTS),
+                    out=grouped_words[:, :, b, :, :].rearrange("p t w (e i) -> p t w e i", i=2),
+                    in_=xt[:].rearrange("p i e (t w) -> p t w e i", t=HALF_STEPS),
                 )
 
             def quantise_x(h):
@@ -237,11 +240,11 @@ def tile_attgcn_pa_t_kernel(
                 return lambda: multiply(label, m)
 
             return [
-                lambda: transpose(0, 0),
-                lambda: transpose(0, 1),
-                calls(lambda: quantise_x(0), lambda: transpose(1, 0)),
-                lambda: transpose(1, 1),
+                calls(lambda: transpose(0, 0), lambda: transpose(0, 1)),
+                calls(lambda: transpose(1, 0), lambda: transpose(1, 1)),
+                lambda: quantise_x(0),
                 lambda: quantise_x(1),
+                lambda: None,
                 tensor_sums("phi", 0),
                 tensor_sums("phi", 1),
                 tensor_sums("phi", 2),
@@ -257,34 +260,26 @@ def tile_attgcn_pa_t_kernel(
         for piece in head[:5]:
             piece()
         weight_q["theta"] = quantise_weight(theta_raw, "theta")
+        kappa_codes, kappa_scales = quantise_weight(kappa_raw, "kappa")
         for piece in head[5:9]:
             piece()
-        kappa_codes, kappa_scales = quantise_weight(kappa_raw, "kappa")
         a_plus = keep.tile([P, PACK, JOINTS * JOINTS], F32)
-        for piece in head[9:-1]:
+        for piece in head[9:]:
             piece()
-        for m in range(PACK):
-            nc.vector.tensor_scalar(
-                out=a_plus[:, m, :], in0=a_bf16[:, m, :], scalar1=1.0, scalar2=lam_bias[:, m : m + 1],
-                op0=ALU.mult, op1=ALU.add,
+
+        def add_kappa_bias(m, half):
+            pairs = slice(half * PAIRS, (half + 1) * PAIRS)
+            nc.scalar.activation(
+                out=a_plus[:, m, pairs],
+                in_=a_bf16[:, m, pairs],
+                func=ACT.Identity,
+                bias=lam_bias[:, m : m + 1],
+                scale=1.0,
             )
-        head[-1]()
 
         def split_terms(b):
             g, first = b // GROUP, (b % GROUP) * JOINTS
             terms = terms_tiles[b % 2]
-            th = th_sbuf[g][:, first : first + JOINTS, :].rearrange("p v m -> p m v")
-            p = p_sbuf[g][:, first : first + JOINTS, :].rearrange("p (o u) m -> p o m u", u=OCTET)
-            th_shape = [P, OCTETS, PACK, JOINTS]
-
-            def all_octets(ap):
-                return ap.unsqueeze(1).to_broadcast(th_shape)
-
-            def th_term(i):
-                return terms[:, :, :, i * JOINTS : (i + 1) * JOINTS]
-
-            def p_term(i):
-                return terms[:, :, :, P_ROW + i * OCTET : P_ROW + (i + 1) * OCTET]
 
             def as_bf16(out, in_):
                 nc.gpsimd.tensor_scalar(out=out, in0=in_, scalar1=1.0, scalar2=0.0, op0=ALU.mult, op1=ALU.add)
@@ -292,16 +287,34 @@ def tile_attgcn_pa_t_kernel(
             def minus(out, in0, in1):
                 nc.gpsimd.tensor_tensor(out=out, in0=in0, in1=in1, op=ALU.subtract)
 
+            def split_in_three(value, rest, term):
+                as_bf16(term(0), value)
+                minus(rest, value, term(0))
+                as_bf16(term(1), rest)
+                minus(term(2), rest, term(1))
+
+            th_terms = split.tile([P, PACK, P_ROW], BF16)
             th_rest = split.tile([P, PACK, JOINTS], F32)
+            split_in_three(
+                th_sbuf[g][:, first : first + JOINTS, :].rearrange("p v m -> p m v"),
+                th_rest[:],
+                lambda i: th_terms[:, :, i * JOINTS : (i + 1) * JOINTS],
+            )
+            th_terms_of[b] = th_terms
             p_rest = split.tile([P, OCTETS, PACK, OCTET], F32)
-            as_bf16(th_term(0), all_octets(th))
-            as_bf16(p_term(0), p)
-            minus(th_rest[:], th, terms[:, 0, :, 0:JOINTS])
-            minus(p_rest[:], p, p_term(0))
-            as_bf16(th_term(1), all_octets(th_rest[:]))
-            as_bf16(p_term(1), p_rest[:])
-            minus(th_term(2), all_octets(th_rest[:]), all_octets(terms[:, 0, :, JOINTS : 2 * JOINTS]))
-            minus(p_term(2), p_rest[:], p_term(1))
+            split_in_three(
+                p_sbuf[g][:, first : first + JOINTS, :].rearrange("p (o u) m -> p o m u", u=OCTET),
+                p_rest[:],
+                lambda i: terms[:, :, :, P_ROW + i * OCTET : P_ROW + (i + 1) * OCTET],
+            )
+
+        th_terms_of = {}
+
+        def spread_terms(b):
+            nc.scalar.copy(
+                out=terms_tiles[b % 2][:, :, :, 0:P_ROW],
+                in_=th_terms_of[b][:].unsqueeze(1).to_broadcast([P, OCTETS, PACK, P_ROW]),
+            )
 
         operands_of = {}
 
@@ -318,15 +331,25 @@ def tile_attgcn_pa_t_kernel(
 
         differences, squashed, codes_of, acc_of = {}, {}, {}, {}
 
+        p_psum = {}
+
+        def p_to_psum(g):
+            bank = ps_keep.tile([P, COLS * PACK], F32)
+            nc.tensor.matmul(
+                bank[:], lhsT=ident[:], rhs=p_sbuf[g][:].rearrange("p c m -> p (c m)"), start=True, stop=True
+            )
+            p_psum[g] = bank[:].rearrange("p (c m) -> p c m", m=PACK)
+
         def subtract(quad, engine):
             b = quad // BATCH_QUADS
             g, first = b // GROUP, (b % GROUP) * JOINTS
             u0 = first + (quad % BATCH_QUADS) * QUAD
+            p = p_psum[g] if engine is nc.vector else p_sbuf[g][:]
             diff = quads.tile([P, QUAD, JOINTS, PACK], F32)
             shape = [P, QUAD, JOINTS, PACK]
             engine.tensor_tensor(
                 out=diff[:],
-                in0=p_sbuf[g][:, u0 : u0 + QUAD, :].unsqueeze(2).to_broadcast(shape),
+                in0=p[:, u0 : u0 + QUAD, :].unsqueeze(2).to_broadcast(shape),
                 in1=th_sbuf[g][:, first : first + JOINTS, :].unsqueeze(1).to_broadcast(shape),
                 op=ALU.subtract,
             )
@@ -399,26 +422,32 @@ def tile_attgcn_pa_t_kernel(
         def at(step, call):
             extra.setdefault(step, []).append(call)
 
-        for g, first_step in ((1, -9), (2, 3), (3, 20)):
+        for g, first_step in ((1, -8), (2, 5), (3, 20)):
             pieces = stage1_pieces(g)
             for i in range(len(pieces)):
                 at(first_step + i, pieces[i])
+        for g in range(N_GROUPS):
+            at((-11, 8, 24, 40)[g], lambda g=g: p_to_psum(g))
+        for m in range(PACK):
+            at(-12 + m, lambda m=m: add_kappa_bias(m, 0))
+            at(2 + m, lambda m=m: add_kappa_bias(m, 1))
         for b in TENSOR_BATCHES:
             first = b * BATCH_QUADS
-            at(first - 15, lambda b=b: split_terms(b))
+            at(first - 14, lambda b=b: split_terms(b))
+            at(first - 10 - 1, lambda b=b: spread_terms(b))
             at(first - 10, lambda b=b: transpose_terms(b, 0))
-            at(first - 9, lambda b=b: transpose_terms(b, 1))
+            at(first - 10 + 1, lambda b=b: transpose_terms(b, 1))
 
         def on_tensor(quad):
             return 0 <= quad < N_QUADS and quad // BATCH_QUADS in TENSOR_BATCHES
 
-        def on_gpsimd(quad):
-            return 0 <= quad < N_QUADS and not on_tensor(quad) and quad not in VECTOR_QUADS
+        def direct(quad, parity):
+            return 0 <= quad < N_QUADS and not on_tensor(quad) and quad % 2 == parity
 
-        for step in range(-10, N_QUADS):
-            if on_gpsimd(step + 10):
+        for step in range(-12, N_QUADS):
+            if direct(step + 10, 1):
                 subtract(step + 10, nc.gpsimd)
-            if step + 7 in VECTOR_QUADS:
+            if direct(step + 7, 0):
                 subtract(step + 7, nc.vector)
             if (step + 2) % UNIT_QUADS == 0 and 0 <= step + 2 < N_QUADS:
                 quantise((step + 2) // UNIT_QUADS)

@@ -37,7 +37,7 @@ OCTETS = JOINTS // OCTET
 TERMS = 3
 P_ROW = TERMS * JOINTS
 
-TENSOR_BATCHES = (3, 5, 7)
+TENSOR_BATCHES = (5, 7)
 
 FLOPS = 2 * BATCH * STEPS * JOINTS * WIDTH * 2 * WIDTH + 2 * BATCH * JOINTS * JOINTS * WIDTH * WIDTH
 
@@ -96,9 +96,9 @@ def tile_attgcn_pa_t_kernel(
         x_rows = [load_x(0)]
         theta_raw = load_weight(theta_w, "theta", 2)
         kappa_raw = load_weight(kappa_w, "kappa", 1)
-        x_rows.append(load_x(1))
         a_bf16 = keep.tile([P, PACK, JOINTS * JOINTS], BF16)
         nc.sync.dma_start(out=a_bf16[:], in_=A.rearrange("(q m) u v -> q m (u v)", m=PACK))
+        x_rows.append(load_x(1))
         for g in range(2, N_GROUPS):
             x_rows.append(load_x(g))
 
@@ -267,14 +267,21 @@ def tile_attgcn_pa_t_kernel(
         for piece in head[9:]:
             piece()
 
-        def add_kappa_bias(m, half):
-            pairs = slice(half * PAIRS, (half + 1) * PAIRS)
+        def add_kappa_bias(m):
             nc.scalar.activation(
-                out=a_plus[:, m, pairs],
-                in_=a_bf16[:, m, pairs],
+                out=a_plus[:, m, 0:PAIRS],
+                in_=a_bf16[:, m, 0:PAIRS],
                 func=ACT.Identity,
                 bias=lam_bias[:, m : m + 1],
                 scale=1.0,
+            )
+            nc.gpsimd.tensor_scalar(
+                out=a_plus[:, m, PAIRS:],
+                in0=a_bf16[:, m, PAIRS:],
+                scalar1=1.0,
+                scalar2=lam_bias[:, m : m + 1],
+                op0=ALU.mult,
+                op1=ALU.add,
             )
 
         def split_terms(b):
@@ -344,7 +351,7 @@ def tile_attgcn_pa_t_kernel(
             b = quad // BATCH_QUADS
             g, first = b // GROUP, (b % GROUP) * JOINTS
             u0 = first + (quad % BATCH_QUADS) * QUAD
-            p = p_psum[g] if engine is nc.vector else p_sbuf[g][:]
+            p = p_psum[g] if engine is nc.vector and g in p_psum else p_sbuf[g][:]
             diff = quads.tile([P, QUAD, JOINTS, PACK], F32)
             shape = [P, QUAD, JOINTS, PACK]
             engine.tensor_tensor(
@@ -422,27 +429,29 @@ def tile_attgcn_pa_t_kernel(
         def at(step, call):
             extra.setdefault(step, []).append(call)
 
-        for g, first_step in ((1, -8), (2, 5), (3, 20)):
+        for g, steps in ((1, (-8, -7, -6, -5, -4, -3, -2, -1, 0, 1, 2, 3, 4, 5)), (2, (5, 6, 7, 8, 9, 10, 11, 12, 13, 14, 15, 16, 17, 19)), (3, (17, 18, 19, 20, 21, 22, 23, 24, 25, 26, 27, 28, 29, 30))):
             pieces = stage1_pieces(g)
             for i in range(len(pieces)):
-                at(first_step + i, pieces[i])
-        for g in range(N_GROUPS):
-            at((-11, 8, 24, 40)[g], lambda g=g: p_to_psum(g))
+                at(steps[i], pieces[i])
+        at(-11, lambda: p_to_psum(0))
+        at(8, lambda: p_to_psum(1))
+        at(24, lambda: p_to_psum(2))
+        at(40, lambda: p_to_psum(3))
         for m in range(PACK):
-            at(-12 + m, lambda m=m: add_kappa_bias(m, 0))
-            at(2 + m, lambda m=m: add_kappa_bias(m, 1))
+            add_kappa_bias(m)
         for b in TENSOR_BATCHES:
             first = b * BATCH_QUADS
             at(first - 14, lambda b=b: split_terms(b))
-            at(first - 10 - 1, lambda b=b: spread_terms(b))
-            at(first - 10, lambda b=b: transpose_terms(b, 0))
-            at(first - 10 + 1, lambda b=b: transpose_terms(b, 1))
+            at(first - 11 - 2, lambda b=b: spread_terms(b))
+            at(first - 11, lambda b=b: transpose_terms(b, 0))
+            at(first - 11 + 1, lambda b=b: transpose_terms(b, 1))
 
         def on_tensor(quad):
             return 0 <= quad < N_QUADS and quad // BATCH_QUADS in TENSOR_BATCHES
 
         def direct(quad, parity):
-            return 0 <= quad < N_QUADS and not on_tensor(quad) and quad % 2 == parity
+            on_vector = quad < 6 or quad % 8 in (0, 3, 6)
+            return 0 <= quad < N_QUADS and not on_tensor(quad) and on_vector == (parity == 0)
 
         for step in range(-12, N_QUADS):
             if direct(step + 10, 1):

@@ -267,7 +267,7 @@ def tile_attgcn_pa_t_kernel(
         for piece in head[9:]:
             piece()
 
-        def add_kappa_bias(m):
+        def add_kappa_bias_first(m):
             nc.scalar.activation(
                 out=a_plus[:, m, 0:PAIRS],
                 in_=a_bf16[:, m, 0:PAIRS],
@@ -275,13 +275,14 @@ def tile_attgcn_pa_t_kernel(
                 bias=lam_bias[:, m : m + 1],
                 scale=1.0,
             )
-            nc.gpsimd.tensor_scalar(
+
+        def add_kappa_bias_second(m):
+            nc.scalar.activation(
                 out=a_plus[:, m, PAIRS:],
-                in0=a_bf16[:, m, PAIRS:],
-                scalar1=1.0,
-                scalar2=lam_bias[:, m : m + 1],
-                op0=ALU.mult,
-                op1=ALU.add,
+                in_=a_bf16[:, m, PAIRS:],
+                func=ACT.Identity,
+                bias=lam_bias[:, m : m + 1],
+                scale=1.0,
             )
 
         def split_terms(b):
@@ -438,7 +439,8 @@ def tile_attgcn_pa_t_kernel(
         at(24, lambda: p_to_psum(2))
         at(40, lambda: p_to_psum(3))
         for m in range(PACK):
-            add_kappa_bias(m)
+            add_kappa_bias_first(m)
+            at(2 + m, lambda m=m: add_kappa_bias_second(m))
         for b in TENSOR_BATCHES:
             first = b * BATCH_QUADS
             at(first - 14, lambda b=b: split_terms(b))

@@ -82,10 +82,8 @@ def tile_attgcn_pa_t_kernel(
 
         def load_per_channel(vec, label):
             narrow = keep.tile([P, PACK], BF16, name="%s_bf16" % label)
-            nc.scalar.dma_start(out=narrow[:], in_=vec.rearrange("(q m) -> q m", m=PACK))
-            wide = keep.tile([P, PACK], F32, name="%s_f32" % label)
-            nc.vector.tensor_copy(out=wide[:], in_=narrow[:])
-            return wide
+            nc.sync.dma_start(out=narrow[:], in_=vec.rearrange("(q m) -> q m", m=PACK))
+            return narrow
 
         ident = keep.tile([P, P], F32)
         make_identity(nc, ident[:])
@@ -95,25 +93,17 @@ def tile_attgcn_pa_t_kernel(
         phi_raw = load_weight(phi_w, "phi", 2)
         x_rows = [load_x(0)]
         theta_raw = load_weight(theta_w, "theta", 2)
+        lam_bf16 = keep.tile([P, 1], BF16)
+        nc.sync.dma_start(out=lam_bf16[:], in_=lam.partition_broadcast(P))
+        kappa_narrow = load_per_channel(kappa_b, "kappa_b")
+        phi_narrow = load_per_channel(phi_b, "phi_b")
+        theta_narrow = load_per_channel(theta_b, "theta_b")
         kappa_raw = load_weight(kappa_w, "kappa", 1)
         a_bf16 = keep.tile([P, PACK, JOINTS * JOINTS], BF16)
         nc.sync.dma_start(out=a_bf16[:], in_=A.rearrange("(q m) u v -> q m (u v)", m=PACK))
         x_rows.append(load_x(1))
         for g in range(2, N_GROUPS):
             x_rows.append(load_x(g))
-
-        phi_bias = load_per_channel(phi_b, "phi_b")
-        theta_bias = load_per_channel(theta_b, "theta_b")
-        kappa_bias = load_per_channel(kappa_b, "kappa_b")
-        lam_bf16 = keep.tile([P, 1], BF16)
-        nc.scalar.dma_start(out=lam_bf16[:], in_=lam.partition_broadcast(P))
-        lam_col = keep.tile([P, 1], F32)
-        nc.vector.tensor_copy(out=lam_col[:], in_=lam_bf16[:])
-        bias16 = keep.tile([P, PACK], F32)
-        nc.vector.tensor_sub(out=bias16[:], in0=theta_bias[:], in1=phi_bias[:])
-        nc.vector.tensor_scalar_mul(out=bias16[:], in0=bias16[:], scalar1=float(STEPS))
-        lam_bias = keep.tile([P, PACK], F32)
-        nc.vector.tensor_scalar_mul(out=lam_bias[:], in0=kappa_bias[:], scalar1=lam_col[:, 0:1])
 
         th_rows = keep.tile([P, JOINTS], F32)
         p_rows = keep.tile([P, OCTET], F32)
@@ -260,6 +250,13 @@ def tile_attgcn_pa_t_kernel(
         for piece in head[:5]:
             piece()
         weight_q["theta"] = quantise_weight(theta_raw, "theta")
+        lam_col = keep.tile([P, 1], F32)
+        nc.vector.tensor_copy(out=lam_col[:], in_=lam_bf16[:])
+        lam_bias = keep.tile([P, PACK], F32)
+        nc.vector.tensor_scalar_mul(out=lam_bias[:], in0=kappa_narrow[:], scalar1=lam_col[:, 0:1])
+        bias16 = keep.tile([P, PACK], F32)
+        nc.vector.tensor_tensor(out=bias16[:], in0=theta_narrow[:], in1=phi_narrow[:], op=ALU.subtract)
+        nc.vector.tensor_scalar_mul(out=bias16[:], in0=bias16[:], scalar1=float(STEPS))
         kappa_codes, kappa_scales = quantise_weight(kappa_raw, "kappa")
         for piece in head[5:9]:
             piece()
@@ -430,11 +427,11 @@ def tile_attgcn_pa_t_kernel(
         def at(step, call):
             extra.setdefault(step, []).append(call)
 
-        for g, steps in ((1, (-8, -7, -6, -5, -4, -3, -2, -1, 0, 1, 2, 3, 4, 5)), (2, (5, 6, 7, 8, 9, 10, 11, 12, 13, 14, 15, 16, 17, 19)), (3, (17, 18, 19, 20, 21, 22, 23, 24, 25, 26, 27, 28, 29, 30))):
+        for g, steps in ((1, (-8, -8, -7, -6, -5, -5, -4, -3, -2, -2, -1, 0, 1, 2)), (2, (5, 6, 7, 8, 9, 10, 11, 12, 13, 14, 15, 16, 17, 19)), (3, (17, 18, 19, 20, 21, 22, 23, 24, 25, 26, 27, 28, 29, 30))):
             pieces = stage1_pieces(g)
             for i in range(len(pieces)):
                 at(steps[i], pieces[i])
-        at(-11, lambda: p_to_psum(0))
+        at(-6, lambda: p_to_psum(0))
         at(8, lambda: p_to_psum(1))
         at(24, lambda: p_to_psum(2))
         at(40, lambda: p_to_psum(3))
@@ -443,7 +440,7 @@ def tile_attgcn_pa_t_kernel(
             at(2 + m, lambda m=m: add_kappa_bias_second(m))
         for b in TENSOR_BATCHES:
             first = b * BATCH_QUADS
-            at(first - 14, lambda b=b: split_terms(b))
+            at(first - 16, lambda b=b: split_terms(b))
             at(first - 11 - 2, lambda b=b: spread_terms(b))
             at(first - 11, lambda b=b: transpose_terms(b, 0))
             at(first - 11 + 1, lambda b=b: transpose_terms(b, 1))

from contextlib import ExitStack

import concourse.mybir as mybir
from concourse.masks import make_identity

F32 = mybir.dt.float32
BF16 = mybir.dt.bfloat16
U32 = mybir.dt.uint32
U8 = mybir.dt.uint8
FP8X4 = mybir.dt.float8_e4m3fn_x4
ALU = mybir.AluOpType
ACT = mybir.ActivationFunctionType
ENGINE = mybir.EngineType

BATCH, STEPS, JOINTS, WIDTH = 8, 16, 32, 512
P = 128
PACK = 4
assert P * PACK == WIDTH

GROUP = 2
N_GROUPS = BATCH // GROUP
COLS = GROUP * JOINTS
PASS_STEPS = P // COLS
PASSES = STEPS // PASS_STEPS
HALF_STEPS = 8

QUAD = 4
QUAD_PAIRS = QUAD * JOINTS
QUAD_WIDTH = QUAD_PAIRS * PACK
UNIT_QUADS = 4
PAIRS = UNIT_QUADS * QUAD_PAIRS
BATCH_QUADS = JOINTS // QUAD
N_QUADS = BATCH * BATCH_QUADS
N_UNITS = N_QUADS // UNIT_QUADS
OCTET = 8
OCTETS = JOINTS // OCTET
TERMS = 3
P_ROW = TERMS * JOINTS

TENSOR_BATCHES = (5, 7)

FLOPS = 2 * BATCH * STEPS * JOINTS * WIDTH * 2 * WIDTH + 2 * BATCH * JOINTS * JOINTS * WIDTH * WIDTH


def tile_attgcn_pa_t_kernel(
    tc, x, A, lam, phi_w, phi_b, theta_w, theta_b, kappa_w, kappa_b, out
):
    nc = tc.nc
    with ExitStack() as stack:
        keep = stack.enter_context(tc.tile_pool(name="keep", bufs=1))
        x_pool = stack.enter_context(tc.tile_pool(name="x_rows", bufs=N_GROUPS * GROUP * 2))
        stage = stack.enter_context(tc.tile_pool(name="stage", bufs=2))
        split = stack.enter_context(tc.tile_pool(name="split", bufs=2))
        quads = stack.enter_context(tc.tile_pool(name="quads", bufs=8))
        work = stack.enter_context(tc.tile_pool(name="work", bufs=4))
        results = stack.enter_context(tc.tile_pool(name="results", bufs=12))
        ps_keep = stack.enter_context(tc.psum_pool(name="ps_keep", bufs=1))
        ps_out = stack.enter_context(tc.psum_pool(name="ps_out", bufs=3))
        ps_bank = stack.enter_context(tc.psum_pool(name="ps_bank", bufs=4))

        def load_weight(w, label, halves):
            raw = keep.tile([P, PACK, WIDTH], BF16, name="%s_raw" % label)
            nc.sync.dma_start(
                out=raw[:].rearrange("p (i e) c -> p i e c", i=halves),
                in_=w.rearrange("(i p e) c -> p i e c", i=halves, p=P),
            )
            return raw

        def load_x(g):
            tiles = {}
            for h in range(STEPS // HALF_STEPS):
                for b in range(GROUP):
                    rows = x_pool.tile([P, 2, WIDTH], BF16)
                    nc.sync.dma_start(
                        out=rows[:],
                        in_=x[g * GROUP + b, h * HALF_STEPS : (h + 1) * HALF_STEPS].rearrange(
                            "t (w e) f -> (t w) e f", e=2
                        ),
                    )
                    tiles[h, b] = rows
            return tiles

        def load_per_channel(vec, label):
            narrow = keep.tile([P, PACK], BF16, name="%s_bf16" % label)
            nc.sync.dma_start(out=narrow[:], in_=vec.rearrange("(q m) -> q m", m=PACK))
            return narrow

        ident = keep.tile([P, P], F32)
        make_identity(nc, ident[:])
        ident_bf16 = keep.tile([P, P], BF16)
        nc.gpsimd.tensor_copy(out=ident_bf16[:], in_=ident[:])

        phi_raw = load_weight(phi_w, "phi", 2)
        x_rows = [load_x(0)]
        theta_raw = load_weight(theta_w, "theta", 2)
        lam_bf16 = keep.tile([P, 1], BF16)
        nc.sync.dma_start(out=lam_bf16[:], in_=lam.partition_broadcast(P))
        kappa_narrow = load_per_channel(kappa_b, "kappa_b")
        phi_narrow = load_per_channel(phi_b, "phi_b")
        theta_narrow = load_per_channel(theta_b, "theta_b")
        kappa_raw = load_weight(kappa_w, "kappa", 1)
        a_bf16 = keep.tile([P, PACK, JOINTS * JOINTS], BF16)
        nc.sync.dma_start(out=a_bf16[:], in_=A.rearrange("(q m) u v -> q m (u v)", m=PACK))
        x_rows.append(load_x(1))
        for g in range(2, N_GROUPS):
            x_rows.append(load_x(g))

        th_rows = keep.tile([P, JOINTS], F32)
        p_rows = keep.tile([P, OCTET], F32)
        for rows, first, width in ((th_rows, 0, JOINTS), (p_rows, P_ROW, OCTET)):
            nc.gpsimd.tensor_tensor(
                out=rows[:], in0=ident[:, first : first + width], in1=ident[:, first + width : first + 2 * width], op=ALU.add
            )
            nc.gpsimd.tensor_tensor(
                out=rows[:], in0=rows[:], in1=ident[:, first + 2 * width : first + 3 * width], op=ALU.add
            )
        select = keep.tile([P, OCTET, JOINTS], BF16)
        nc.gpsimd.tensor_tensor(
            out=select[:],
            in0=p_rows[:].unsqueeze(2).to_broadcast([P, OCTET, JOINTS]),
            in1=th_rows[:].unsqueeze(1).to_broadcast([P, OCTET, JOINTS]),
            op=ALU.subtract,
        )
        terms_tiles = []
        for i in range(2):
            terms = keep.tile([P, OCTETS, PACK, P], BF16, name="terms%d" % i)
            nc.gpsimd.memset(terms[:, :, :, P_ROW + TERMS * OCTET :], 0.0)
            terms_tiles.append(terms)

        stack.enter_context(tc.manual_schedule(engines={ENGINE.PE, ENGINE.DVE, ENGINE.Activation, ENGINE.Pool}))

        def quantise_weight(raw, label):
            grouped = stage.tile([P, PACK, P, PACK], BF16, align_bytes=64, tag="grouped")
            nc.vector.tensor_copy(out=grouped[:], in_=raw[:].rearrange("p j (q m) -> p m q j", m=PACK))
            codes = keep.tile([P, PACK, P], U32, align_bytes=64, name="%s_codes" % label)
            scales = keep.tile([P, PACK, P], U8, align_bytes=64, name="%s_scales" % label)
            nc.vector.quantize_mx(
                out=codes[:].rearrange("p m q -> p (m q)").bitcast(FP8X4),
                scales=scales[:].rearrange("p m q -> p (m q)"),
                in_=grouped[:].rearrange("p m q j -> p (m q j)"),
            )
            return codes, scales

        weight_q = {"phi": quantise_weight(phi_raw, "phi")}

        p_sbuf, th_sbuf = [], []
        for g in range(N_GROUPS):
            p_tile = keep.tile([P, COLS, PACK], F32, name="p%d" % g)
            th_tile = keep.tile([P, COLS, PACK], F32, name="th%d" % g)
            p_sbuf.append(p_tile)
            th_sbuf.append(th_tile)

        def stage1_pieces(g):
            x_codes = keep.tile([P, PASSES, P], U32, align_bytes=64, name="x_codes%d" % g)
            x_scales = keep.tile([P, PASSES, P], U8, align_bytes=64, name="x_scales%d" % g)
            grouped_of, sums_of = {}, {}

            def transpose(h, b):
                if b == 0:
                    grouped = stage.tile([P, HALF_STEPS, GROUP, JOINTS, PACK], BF16, align_bytes=64, tag="grouped")
                    grouped_of[h] = grouped[:].rearrange("p t b v j -> p (t b v j)")
                grouped_words = grouped_of[h].bitcast(F32).rearrange(
                    "p (t b w k) -> p t b w k", t=HALF_STEPS, b=GROUP, w=JOINTS // 2
                )
                xt = ps_bank.tile([P, 2, 2, P], F32, tag="bank")
                for e in range(2):
                    words = x_rows[g][h, b][:, e, :].bitcast(F32).rearrange("p (i w) -> p i w", i=2)
                    for i in range(2):
                        nc.tensor.transpose(xt[:, i, e, :], words[:, i, :], ident[:])
                nc.scalar.copy(
                    out=grouped_words[:, :, b, :, :].rearrange("p t w (e i) -> p t w e i", i=2),
                    in_=xt[:].rearrange("p i e (t w) -> p t w e i", t=HALF_STEPS),
                )

            def quantise_x(h):
                half = slice(h * PASSES // 2, (h + 1) * PASSES // 2)
                nc.vector.quantize_mx(
                    out=x_codes[:, half, :].rearrange("p t c -> p (t c)").bitcast(FP8X4),
                    scales=x_scales[:, half, :].rearrange("p t c -> p (t c)"),
                    in_=grouped_of[h],
                )

            def multiply(label, m):
                w_codes, w_scales = weight_q[label]
                if m == 0:
                    sums = ps_bank.tile([P, PACK, P], F32, tag="bank")
                    sums_of[label] = sums
                for k in range(PASSES):
                    nc.tensor.matmul_mx(
                        out=sums_of[label][:, m, :],
                        lhsT=w_codes[:, m, :].bitcast(FP8X4),
                        lhsT_scale=w_scales[:, m, :],
                        rhs=x_codes[:, k, :].bitcast(FP8X4),
                        rhs_scale=x_scales[:, k, :],
                        start=(k == 0),
                        stop=(k == PASSES - 1),
                    )

            def parity(label, i):
                return sums_of[label][:, :, i * COLS : (i + 1) * COLS].rearrange("p m c -> p c m")

            def copy_odd_phi():
                odd = split.tile([P, COLS, PACK], F32)
                nc.scalar.copy(out=odd[:], in_=parity("phi", 1))
                sums_of["odd phi"] = odd

            def add_phi():
                nc.vector.tensor_tensor(
                    out=p_sbuf[g][:], in0=parity("phi", 0), in1=sums_of["odd phi"][:], op=ALU.add
                )

            def add_theta():
                odd_th = split.tile([P, COLS, PACK], F32)
                nc.vector.tensor_tensor(
                    out=odd_th[:],
                    in0=parity("theta", 1),
                    in1=bias16[:].unsqueeze(1).to_broadcast([P, COLS, PACK]),
                    op=ALU.add,
                )
                nc.vector.tensor_tensor(out=th_sbuf[g][:], in0=parity("theta", 0), in1=odd_th[:], op=ALU.add)

            def calls(*functions):
                def run():
                    for f in functions:
                        f()

                return run

            def tensor_sums(label, m):
                return lambda: multiply(label, m)

            return [
                calls(lambda: transpose(0, 0), lambda: transpose(0, 1)),
                calls(lambda: transpose(1, 0), lambda: transpose(1, 1)),
                lambda: quantise_x(0),
                lambda: quantise_x(1),
                lambda: None,
                tensor_sums("phi", 0),
                tensor_sums("phi", 1),
                tensor_sums("phi", 2),
                tensor_sums("phi", 3),
                calls(copy_odd_phi, tensor_sums("theta", 0)),
                calls(add_phi, tensor_sums("theta", 1)),
                tensor_sums("theta", 2),
                tensor_sums("theta", 3),
                add_theta,
            ]

        head = stage1_pieces(0)
        for piece in head[:5]:
            piece()
        weight_q["theta"] = quantise_weight(theta_raw, "theta")
        lam_col = keep.tile([P, 1], F32)
        nc.vector.tensor_copy(out=lam_col[:], in_=lam_bf16[:])
        lam_bias = keep.tile([P, PACK], F32)
        nc.vector.tensor_scalar_mul(out=lam_bias[:], in0=kappa_narrow[:], scalar1=lam_col[:, 0:1])
        bias16 = keep.tile([P, PACK], F32)
        nc.vector.tensor_tensor(out=bias16[:], in0=theta_narrow[:], in1=phi_narrow[:], op=ALU.subtract)
        nc.vector.tensor_scalar_mul(out=bias16[:], in0=bias16[:], scalar1=float(STEPS))
        kappa_codes, kappa_scales = quantise_weight(kappa_raw, "kappa")
        for piece in head[5:9]:
            piece()
        a_plus = keep.tile([P, PACK, JOINTS * JOINTS], F32)
        for piece in head[9:]:
            piece()

        def add_kappa_bias_first(m):
            nc.scalar.activation(
                out=a_plus[:, m, 0:PAIRS],
                in_=a_bf16[:, m, 0:PAIRS],
                func=ACT.Identity,
                bias=lam_bias[:, m : m + 1],
                scale=1.0,
            )

        def add_kappa_bias_second(m):
            nc.scalar.activation(
                out=a_plus[:, m, PAIRS:],
                in_=a_bf16[:, m, PAIRS:],
                func=ACT.Identity,
                bias=lam_bias[:, m : m + 1],
                scale=1.0,
            )

        def split_terms(b):
            g, first = b // GROUP, (b % GROUP) * JOINTS
            terms = terms_tiles[b % 2]

            def as_bf16(out, in_):
                nc.gpsimd.tensor_scalar(out=out, in0=in_, scalar1=1.0, scalar2=0.0, op0=ALU.mult, op1=ALU.add)

            def minus(out, in0, in1):
                nc.gpsimd.tensor_tensor(out=out, in0=in0, in1=in1, op=ALU.subtract)

            def split_in_three(value, rest, term):
                as_bf16(term(0), value)
                minus(rest, value, term(0))
                as_bf16(term(1), rest)
                minus(term(2), rest, term(1))

            th_terms = split.tile([P, PACK, P_ROW], BF16)
            th_rest = split.tile([P, PACK, JOINTS], F32)
            split_in_three(
                th_sbuf[g][:, first : first + JOINTS, :].rearrange("p v m -> p m v"),
                th_rest[:],
                lambda i: th_terms[:, :, i * JOINTS : (i + 1) * JOINTS],
            )
            th_terms_of[b] = th_terms
            p_rest = split.tile([P, OCTETS, PACK, OCTET], F32)
            split_in_three(
                p_sbuf[g][:, first : first + JOINTS, :].rearrange("p (o u) m -> p o m u", u=OCTET),
                p_rest[:],
                lambda i: terms[:, :, :, P_ROW + i * OCTET : P_ROW + (i + 1) * OCTET],
            )

        th_terms_of = {}

        def spread_terms(b):
            nc.scalar.copy(
                out=terms_tiles[b % 2][:, :, :, 0:P_ROW],
                in_=th_terms_of[b][:].unsqueeze(1).to_broadcast([P, OCTETS, PACK, P_ROW]),
            )

        operands_of = {}

        def transpose_terms(b, pair):
            if pair == 0:
                operands = split.tile([P, OCTETS, PACK, P], BF16)
                operands_of[b] = operands
            o = 2 * pair
            bank = ps_bank.tile([P, 2, PACK, P], BF16, tag="bank")
            for i in range(2):
                for m in range(PACK):
                    nc.tensor.transpose(bank[:, i, m, :], terms_tiles[b % 2][:, o + i, m, :], ident_bf16[:])
            nc.scalar.copy(out=operands_of[b][:, o : o + 2], in_=bank[:])

        differences, squashed, codes_of, acc_of = {}, {}, {}, {}

        p_psum = {}

        def p_to_psum(g):
            bank = ps_keep.tile([P, COLS * PACK], F32)
            nc.tensor.matmul(
                bank[:], lhsT=ident[:], rhs=p_sbuf[g][:].rearrange("p c m -> p (c m)"), start=True, stop=True
            )
            p_psum[g] = bank[:].rearrange("p (c m) -> p c m", m=PACK)

        def subtract(quad, engine):
            b = quad // BATCH_QUADS
            g, first = b // GROUP, (b % GROUP) * JOINTS
            u0 = first + (quad % BATCH_QUADS) * QUAD
            p = p_psum[g] if engine is nc.vector and g in p_psum else p_sbuf[g][:]
            diff = quads.tile([P, QUAD, JOINTS, PACK], F32)
            shape = [P, QUAD, JOINTS, PACK]
            engine.tensor_tensor(
                out=diff[:],
                in0=p[:, u0 : u0 + QUAD, :].unsqueeze(2).to_broadcast(shape),
                in1=th_sbuf[g][:, first : first + JOINTS, :].unsqueeze(1).to_broadcast(shape),
                op=ALU.subtract,
            )
            differences[quad] = diff[:].rearrange("p u v m -> p (u v m)")

        def multiply_terms(quad):
            b = quad // BATCH_QUADS
            octet, half = divmod(quad % BATCH_QUADS, OCTET // QUAD)
            bank = ps_bank.tile([P, PACK, QUAD_PAIRS], F32, tag="bank")
            for m in range(PACK):
                nc.tensor.matmul(
                    bank[:, m, :],
                    lhsT=operands_of[b][:, octet, m, :],
                    rhs=select[:, half * QUAD : (half + 1) * QUAD, :].rearrange("p u v -> p (u v)"),
                    start=True,
                    stop=True,
                )
            differences[quad] = bank[:].rearrange("p m n -> p n m")

        def squash(quad):
            unit, i = divmod(quad, UNIT_QUADS)
            if i == 0:
                f_bf16 = work.tile([P, PAIRS, PACK], BF16, align_bytes=64)
                squashed[unit] = f_bf16
            f_quad = squashed[unit][:, i * QUAD_PAIRS : (i + 1) * QUAD_PAIRS, :]
            if quad // BATCH_QUADS not in TENSOR_BATCHES:
                f_quad = f_quad.rearrange("p n m -> p (n m)")
            nc.scalar.activation(out=f_quad, in_=differences[quad], func=ACT.Tanh, scale=1.0 / STEPS)

        def quantise(unit):
            f_codes = work.tile([P, PAIRS], U32, align_bytes=64)
            f_scales = work.tile([P, PAIRS], U8, align_bytes=64)
            nc.vector.quantize_mx(
                out=f_codes[:].bitcast(FP8X4), scales=f_scales[:], in_=squashed[unit][:].rearrange("p n m -> p (n m)")
            )
            codes_of[unit] = (f_codes, f_scales)

        def multiply_kappa(step):
            unit, m = divmod(step, PACK)
            f_codes, f_scales = codes_of[unit]
            acc = ps_out.tile([P, PAIRS], F32)
            nc.tensor.matmul_mx(
                out=acc[:],
                lhsT=kappa_codes[:, m, :].bitcast(FP8X4),
                lhsT_scale=kappa_scales[:, m, :],
                rhs=f_codes[:].bitcast(FP8X4),
                rhs_scale=f_scales[:],
                start=True,
                stop=True,
            )
            acc_of[step] = acc

        def finish(step):
            unit, m = divmod(step, PACK)
            b, half = divmod(unit, 2)
            pairs = slice(half * PAIRS, (half + 1) * PAIRS)
            result = results.tile([P, PAIRS], F32)
            nc.vector.scalar_tensor_tensor(
                out=result[:],
                in0=acc_of[step][:],
                scalar=lam_col[:, 0:1],
                in1=a_plus[:, m, pairs],
                op0=ALU.mult,
                op1=ALU.add,
            )
            nc.sync.dma_start(out=out[b].rearrange("(q m) u v -> q m (u v)", m=PACK)[:, m, pairs], in_=result[:])

        extra = {}

        def at(step, call):
            extra.setdefault(step, []).append(call)

        for g, steps in ((1, (-8, -8, -7, -6, -5, -5, -4, -3, -2, -2, -1, 0, 1, 2)), (2, (5, 6, 7, 8, 9, 10, 11, 12, 13, 14, 15, 16, 17, 19)), (3, (17, 18, 19, 20, 21, 22, 23, 24, 25, 26, 27, 28, 29, 30))):
            pieces = stage1_pieces(g)
            for i in range(len(pieces)):
                at(steps[i], pieces[i])
        at(-6, lambda: p_to_psum(0))
        at(8, lambda: p_to_psum(1))
        at(24, lambda: p_to_psum(2))
        at(40, lambda: p_to_psum(3))
        for m in range(PACK):
            add_kappa_bias_first(m)
            at(2 + m, lambda m=m: add_kappa_bias_second(m))
        for b in TENSOR_BATCHES:
            first = b * BATCH_QUADS
            at(first - 16, lambda b=b: split_terms(b))
            at(first - 11 - 2, lambda b=b: spread_terms(b))
            at(first - 11, lambda b=b: transpose_terms(b, 0))
            at(first - 11 + 1, lambda b=b: transpose_terms(b, 1))

        def on_tensor(quad):
            return 0 <= quad < N_QUADS and quad // BATCH_QUADS in TENSOR_BATCHES

        def direct(quad, parity):
            on_vector = quad < 6 or quad % 8 in (0, 3, 6)
            return 0 <= quad < N_QUADS and not on_tensor(quad) and on_vector == (parity == 0)

        for step in range(-12, N_QUADS):
            if direct(step + 10, 1):
                subtract(step + 10, nc.gpsimd)
            if direct(step + 7, 0):
                subtract(step + 7, nc.vector)
            if (step + 2) % UNIT_QUADS == 0 and 0 <= step + 2 < N_QUADS:
                quantise((step + 2) // UNIT_QUADS)
            if 0 <= step + 1 < N_QUADS:
                multiply_kappa(step + 1)
            if on_tensor(step + 8):
                multiply_terms(step + 8)
            if 0 <= step + 6 < N_QUADS:
                squash(step + 6)
            if step >= 0:
                finish(step)
            for call in extra.get(step, []):
                call()
